import numpy as np
import ml_dtypes


def mxq(x, axis, fmt="e4m3"):
    dtype, down = {"e4m3": (ml_dtypes.float8_e4m3fn, 7), "e5m2": (ml_dtypes.float8_e5m2, 14)}[fmt]
    v = np.moveaxis(np.asarray(x, np.float32).astype(ml_dtypes.bfloat16).astype(np.float64), axis, -1)
    blocks = v.reshape(v.shape[:-1] + (-1, 32))
    amax = np.abs(blocks).max(-1, keepdims=True)
    byte = np.maximum(np.where(amax > 0, np.frexp(amax)[1] - 1 + 127, 0) - down, 1)
    scale = np.exp2(byte - 127.0)
    codes = (blocks / scale).astype(np.float32).astype(dtype).astype(np.float64)
    return np.moveaxis((codes * scale).reshape(v.shape), -1, axis)


WIDE = False


def mx_kscale(k):
    if not WIDE:
        return np.ones(k)
    levels = np.array([10, -10, 5, -5, 0])
    if k % 512:
        return np.exp2(np.random.permutation(np.resize(levels, k // 32))).repeat(32)
    a = np.empty((k // 512, 16))
    for p in range(k // 512):
        a[p, :8] = np.random.permutation(np.resize(levels, 8))
        for g in range(8):
            far = levels[np.abs(levels - a[p, g]) >= 10]
            a[p, g + 8] = far[np.random.randint(len(far))]
    return np.exp2(a.ravel()).repeat(32)


BF16 = ml_dtypes.bfloat16


def bf(x):
    return np.asarray(x, np.float32).astype(BF16)


def f64(x):
    return np.asarray(x).astype(np.float64)


B, L, C = 128, 64, 512
LEVELS = 3
ISQ2 = 0.7071067811865476
LC = L // 2 ** LEVELS


def dwt_haar(a):
    e, o = a[:, 0::2], a[:, 1::2]
    return (e + o) * ISQ2, (e - o) * ISQ2


def idwt_haar(a, d):
    nb, n, c = a.shape
    e = (a + d) * ISQ2
    o = (a - d) * ISQ2
    return np.stack([e, o], axis=2).reshape(nb, 2 * n, c)


def gelu_tanh(v):
    return 0.5 * v * (1.0 + np.tanh(np.sqrt(2.0 / np.pi) * (v + 0.044715 * v**3)))


def mix(a, w):
    return (mxq(a, 2, "e4m3").transpose(1, 0, 2) @ mxq(w, 0, "e4m3").transpose(2, 0, 1)).transpose(1, 0, 2)


def setup_inputs():
    s = mx_kscale(C)
    p = np.minimum(s, 1.0)
    x = np.random.standard_normal((B, LC, C)) * s
    for j in range(LEVELS):
        x = idwt_haar(x, np.random.standard_normal((B, LC * 2 ** j, C)) * (s if j == 0 else p))
    return {"x": bf(x),
            "w_approx": bf(np.random.standard_normal((C, C, LC)) / np.sqrt(C) / s[:, None, None]),
            "w_detail": bf(np.random.standard_normal((C, C, LC)) / np.sqrt(C) / s[:, None, None]),
            "W_skip": bf(np.random.standard_normal((C, C)) / np.sqrt(C) / s[:, None]),
            "b_skip": bf(np.random.standard_normal(C) * 0.3)}


def wavelet_conv1d(x, w_approx, w_detail):
    a = x
    details = []
    for _ in range(LEVELS):
        a, d = dwt_haar(a)
        details.append(d)
    a = mix(a, w_approx)
    details[-1] = mix(details[-1], w_detail)
    for d in reversed(details):
        a = idwt_haar(a, d)
    return a


def reference(x, w_approx, w_detail, W_skip, b_skip):
    x = f64(x)
    y = wavelet_conv1d(x, f64(w_approx), f64(w_detail))
    shortcut = (mxq(x, 2, "e4m3") @ mxq(f64(W_skip), 0, "e4m3")) + f64(b_skip)
    return gelu_tanh(y + shortcut)

@@ -1,0 +1,240 @@
+from contextlib import ExitStack
+
+import concourse.bass as bass
+import concourse.mybir as mybir
+import concourse.tile as tile
+from concourse.masks import make_identity
+
+F32 = mybir.dt.float32
+BF16 = mybir.dt.bfloat16
+U32 = mybir.dt.uint32
+U8 = mybir.dt.uint8
+FP8X4 = mybir.dt.float8_e4m3fn_x4
+ALU = mybir.AluOpType
+ACT = mybir.ActivationFunctionType
+
+P = 128
+C = 512
+UNITS = 8
+R = 0.7071067811865476
+R3 = R * R * R
+FLOPS = 2 * 8192 * 512 * 512 + 2 * 2 * 8 * 128 * 512 * 512
+OC = 256
+
+
+def tile_waveletblock1d_t_kernel(tc, x, w_approx, w_detail, W_skip, b_skip, out):
+    nc = tc.nc
+    with ExitStack() as ctx:
+        const = ctx.enter_context(tc.tile_pool(name="const", bufs=1))
+        xpool = ctx.enter_context(tc.tile_pool(name="xpool", bufs=4))
+        ppool = ctx.enter_context(tc.tile_pool(name="ppool", bufs=1))
+        hpool = ctx.enter_context(tc.tile_pool(name="hpool", bufs=2))
+        gpool = ctx.enter_context(tc.tile_pool(name="gpool", bufs=2))
+        apool = ctx.enter_context(tc.tile_pool(name="apool", bufs=2))
+        keep = ctx.enter_context(tc.tile_pool(name="keep", bufs=3))
+        psum = ctx.enter_context(tc.psum_pool(name="psum", bufs=2))
+
+        ident = const.tile([P, P], F32)
+        make_identity(nc, ident[:])
+        bias_b = const.tile([P, C], BF16)
+        nc.sync.dma_start(out=bias_b[:], in_=b_skip.partition_broadcast(P))
+        bias4 = const.tile([P, C], F32)
+        nc.vector.tensor_scalar(out=bias4[:], in0=bias_b[:], scalar1=4.0, scalar2=None, op0=ALU.mult)
+
+        ws_codes = const.tile([P, C], U32, align_bytes=64)
+        ws_scales = const.tile([P, C], U8, align_bytes=64)
+        w_codes = []
+        w_scales = []
+        for s in range(2):
+            wc = const.tile([P, UNITS * C], U32, align_bytes=64, name="wc%d" % s)
+            wsc = const.tile([P, UNITS * C], U8, align_bytes=64, name="wsc%d" % s)
+            w_codes.append(wc)
+            w_scales.append(wsc)
+
+        xus = {}
+
+        def load_x(u):
+            xu = xpool.tile([P, 8 * C], BF16, tag="xu", name="xu%d" % u)
+            nc.sync.dma_start(out=xu[:], in_=x[:, 8 * u : 8 * u + 8, :].rearrange("b l c -> b (l c)"))
+            xus[u] = xu
+
+        state = {}
+
+        def stage_a(u):
+            xu = xus[u]
+            xv = xu[:].rearrange("p (k two c) -> p k two c", two=2, c=C)
+            pp = ppool.tile([P, 4 * C], F32, tag="pp", name="pp%d" % u)
+            nc.gpsimd.tensor_tensor(
+                out=pp[:].rearrange("p (k c) -> p k c", c=C), in0=xv[:, :, 0, :], in1=xv[:, :, 1, :], op=ALU.add
+            )
+            pv = pp[:].rearrange("p (h two c) -> p h two c", two=2, c=C)
+            s4 = hpool.tile([P, 2 * C], F32, tag="s4", name="s4_%d" % u)
+            nc.gpsimd.tensor_tensor(
+                out=s4[:].rearrange("p (h c) -> p h c", c=C), in0=pv[:, :, 0, :], in1=pv[:, :, 1, :], op=ALU.add
+            )
+            ad = hpool.tile([P, 2 * C], F32, tag="ad", name="ad%d" % u)
+            nc.gpsimd.tensor_tensor(out=ad[:, 0:C], in0=s4[:, 0:C], in1=s4[:, C : 2 * C], op=ALU.add)
+            nc.gpsimd.tensor_tensor(out=ad[:, C : 2 * C], in0=s4[:, 0:C], in1=s4[:, C : 2 * C], op=ALU.subtract)
+            mm = keep.tile([P, 2 * C], F32, tag="mm", name="mm%d" % u)
+            nc.gpsimd.tensor_tensor(
+                out=mm[:].rearrange("p (h c) -> p h c", c=C),
+                in0=s4[:].rearrange("p (h c) -> p h c", c=C),
+                in1=bias4[:].unsqueeze(1).to_broadcast([P, 2, C]),
+                op=ALU.subtract,
+            )
+            xw = xu[:].bitcast(F32)
+            xg = gpool.tile([P, 8 * C], BF16, align_bytes=64, tag="xg", name="xg%d" % u)
+            xgw = xg[:].bitcast(F32)
+            for jp in range(4):
+                tin = psum.tile([P, C], F32, tag="tin", name="tin%d_%d" % (u, jp))
+                for jj in range(2):
+                    j = 2 * jp + jj
+                    for uu in range(2):
+                        nc.tensor.transpose(
+                            tin[:, uu * 256 + jj * P : uu * 256 + jj * P + P],
+                            xw[:, j * 256 + uu : (j + 1) * 256 : 2],
+                            ident[:],
+                        )
+                nc.scalar.copy(
+                    out=xgw[:, jp * C : (jp + 1) * C].rearrange("p (n u) -> p n u", u=2),
+                    in_=tin[:].rearrange("p (u n) -> p n u", u=2),
+                )
+            x_codes = keep.tile([P, 8 * P], U32, align_bytes=64, tag="xc", name="xc%d" % u)
+            x_scales = keep.tile([P, 8 * P], U8, align_bytes=64, tag="xs", name="xs%d" % u)
+            nc.vector.quantize_mx(out=x_codes[:].bitcast(FP8X4), scales=x_scales[:], in_=xg[:])
+            gq = apool.tile([P, 3 * C], BF16, align_bytes=64, tag="gq", name="gq%d" % u)
+            for s in range(2):
+                at = psum.tile([P, C], F32, tag="at", name="at%d_%d" % (u, s))
+                for t in range(4):
+                    nc.tensor.transpose(
+                        at[:, t * P : (t + 1) * P], ad[:, s * C + t : (s + 1) * C : 4], ident[:]
+                    )
+                av = at[:].rearrange("p (t b) -> p b t", t=4)
+                nc.scalar.activation(
+                    out=gq[:, s * C : (s + 1) * C].rearrange("p (b t) -> p b t", t=4), in_=av, func=ACT.Copy, scale=R3
+                )
+                if s == 1:
+                    nc.scalar.activation(
+                        out=gq[:, 2 * C : 3 * C].rearrange("p (b t) -> p b t", t=4), in_=av, func=ACT.Copy, scale=-R3
+                    )
+            a_codes = keep.tile([P, 3 * P], U32, align_bytes=64, tag="ac", name="ac%d" % u)
+            a_scales = keep.tile([P, 3 * P], U8, align_bytes=64, tag="as", name="as%d" % u)
+            nc.vector.quantize_mx(
+                out=a_codes[:, 0 : 2 * P].bitcast(FP8X4), scales=a_scales[:, 0 : 2 * P], in_=gq[:, 0 : 2 * C]
+            )
+            nc.vector.quantize_mx(
+                out=a_codes[:, 2 * P : 3 * P].bitcast(FP8X4), scales=a_scales[:, 2 * P : 3 * P], in_=gq[:, 2 * C : 3 * C]
+            )
+            state[u] = (mm, x_codes, x_scales, a_codes, a_scales)
+
+        wsraw = xpool.tile([P, 8 * C], BF16, tag="xu", name="wsraw")
+        nc.sync.dma_start(
+            out=wsraw[:, 0 : 4 * C].rearrange("p (u r) -> p u r", u=2),
+            in_=W_skip.rearrange("(q u e) o -> q u (e o)", u=2, e=2),
+        )
+        load_x(0)
+        with tc.tile_pool(name="wstage", bufs=2) as wstage:
+            wsg = wstage.tile([P, 8 * OC * 4], BF16, align_bytes=64, tag="wg", name="wsg")
+            nc.vector.tensor_copy(
+                out=wsg[:, 0 : 4 * C].rearrange("p (o t) -> p o t", t=4),
+                in_=wsraw[:, 0 : 4 * C].rearrange("p (t o) -> p o t", t=4),
+            )
+            nc.vector.quantize_mx(out=ws_codes[:].bitcast(FP8X4), scales=ws_scales[:], in_=wsg[:, 0 : 4 * C])
+            raws = []
+            for s, w in enumerate((w_approx, w_detail)):
+                wv = w.rearrange("(p t) o l -> p t o l", t=4)
+                for ch in range(C // OC):
+                    wraw = wstage.tile([P, 4 * OC * 8], BF16, tag="wraw", name="wraw%d_%d" % (s, ch))
+                    nc.sync.dma_start(
+                        out=wraw[:].rearrange("p (t r) -> p t r", t=4),
+                        in_=wv[:, :, ch * OC : (ch + 1) * OC, :].rearrange("p t o l -> p t (o l)"),
+                    )
+                    raws.append((s, ch, wraw))
+                    if ch == 1:
+                        load_x(1 + s)
+            stage_a(0)
+            for s, ch, wraw in raws:
+                wg = wstage.tile([P, 8 * OC * 4], BF16, align_bytes=64, tag="wg", name="wg%d_%d" % (s, ch))
+                src = wraw[:].rearrange("p (t o l) -> p l o t", t=4, l=8)
+                dst = wg[:].rearrange("p (l o t) -> p l o t", l=8, t=4)
+                nc.vector.tensor_copy(out=dst[:, 0:4], in_=src[:, 0:4])
+                nc.scalar.copy(out=dst[:, 5:8], in_=src[:, 5:8])
+                nc.vector.tensor_copy(out=dst[:, 4], in_=src[:, 4])
+                for l in range(8):
+                    nc.vector.quantize_mx(
+                        out=w_codes[s][:, l * C + ch * OC : l * C + (ch + 1) * OC].bitcast(FP8X4),
+                        scales=w_scales[s][:, l * C + ch * OC : l * C + (ch + 1) * OC],
+                        in_=wg[:, l * OC * 4 : (l + 1) * OC * 4],
+                    )
+                if ch == 1:
+                    stage_a(1 + s)
+
+        zpool = ctx.enter_context(tc.tile_pool(name="zpool", bufs=4))
+
+        def stage_b(u):
+            xu = xus[u]
+            mm, x_codes, x_scales, a_codes, a_scales = state[u]
+            cc = hpool.tile([P, 2 * C], F32, tag="cc", name="cc%d" % u)
+            for h in range(2):
+                mx = psum.tile([P, C], F32, tag="mix", name="mix%d_%d" % (u, h))
+                nc.tensor.matmul_mx(
+                    out=mx[:],
+                    lhsT=a_codes[:, 0:P].bitcast(FP8X4),
+                    lhsT_scale=a_scales[:, 0:P],
+                    rhs=w_codes[0][:, u * C : (u + 1) * C].bitcast(FP8X4),
+                    rhs_scale=w_scales[0][:, u * C : (u + 1) * C],
+                    start=True,
+                    stop=False,
+                )
+                nc.tensor.matmul_mx(
+                    out=mx[:],
+                    lhsT=a_codes[:, (1 + h) * P : (2 + h) * P].bitcast(FP8X4),
+                    lhsT_scale=a_scales[:, (1 + h) * P : (2 + h) * P],
+                    rhs=w_codes[1][:, u * C : (u + 1) * C].bitcast(FP8X4),
+                    rhs_scale=w_scales[1][:, u * C : (u + 1) * C],
+                    start=False,
+                    stop=True,
+                )
+                nc.vector.scalar_tensor_tensor(
+                    out=cc[:, h * C : (h + 1) * C],
+                    in0=mx[:],
+                    scalar=-4.0 * R3,
+                    in1=mm[:, h * C : (h + 1) * C],
+                    op0=ALU.mult,
+                    op1=ALU.add,
+                )
+                z = zpool.tile([P, 4 * C], F32, tag="z", name="z%d_%d" % (u, h))
+                nc.vector.scalar_tensor_tensor(
+                    out=z[:].rearrange("p (j c) -> p j c", c=C),
+                    in0=cc[:, h * C : (h + 1) * C].unsqueeze(1).to_broadcast([P, 4, C]),
+                    scalar=-0.25,
+                    in1=xu[:, h * 4 * C : (h + 1) * 4 * C].rearrange("p (j c) -> p j c", c=C),
+                    op0=ALU.mult,
+                    op1=ALU.add,
+                )
+                for jj in range(4):
+                    j = 4 * h + jj
+                    sk = psum.tile([P, C], F32, tag="sk", name="sk%d_%d" % (u, j))
+                    nc.tensor.matmul_mx(
+                        out=sk[:],
+                        lhsT=x_codes[:, j * P : (j + 1) * P].bitcast(FP8X4),
+                        lhsT_scale=x_scales[:, j * P : (j + 1) * P],
+                        rhs=ws_codes[:].bitcast(FP8X4),
+                        rhs_scale=ws_scales[:],
+                        start=True,
+                        stop=True,
+                    )
+                    nc.vector.tensor_tensor(
+                        out=z[:, jj * C : (jj + 1) * C], in0=sk[:], in1=z[:, jj * C : (jj + 1) * C], op=ALU.add
+                    )
+                nc.scalar.activation(out=z[:], in_=z[:], func=ACT.Gelu_apprx_tanh)
+                nc.scalar.dma_start(
+                    out=out[:, 8 * u + 4 * h : 8 * u + 4 * h + 4, :].rearrange("b l o -> b (l o)"), in_=z[:]
+                )
+
+        for u in range(UNITS):
+            if u + 3 < UNITS:
+                load_x(u + 3)
+            stage_b(u)
+            if u + 3 < UNITS:
+                stage_a(u + 3)

@@ -1,8 +1,6 @@
 from contextlib import ExitStack
 
-import concourse.bass as bass
 import concourse.mybir as mybir
-import concourse.tile as tile
 from concourse.masks import make_identity
 
 F32 = mybir.dt.float32
@@ -19,74 +17,57 @@ UNITS = 8
 R = 0.7071067811865476
 R3 = R * R * R
 FLOPS = 2 * 8192 * 512 * 512 + 2 * 2 * 8 * 128 * 512 * 512
-OC = 256
+AHEAD = 3
 
 
 def tile_waveletblock1d_t_kernel(tc, x, w_approx, w_detail, W_skip, b_skip, out):
     nc = tc.nc
     with ExitStack() as ctx:
         const = ctx.enter_context(tc.tile_pool(name="const", bufs=1))
-        xpool = ctx.enter_context(tc.tile_pool(name="xpool", bufs=4))
-        ppool = ctx.enter_context(tc.tile_pool(name="ppool", bufs=1))
-        hpool = ctx.enter_context(tc.tile_pool(name="hpool", bufs=2))
+        xpool = ctx.enter_context(tc.tile_pool(name="xpool", bufs=AHEAD + 1))
         gpool = ctx.enter_context(tc.tile_pool(name="gpool", bufs=2))
-        apool = ctx.enter_context(tc.tile_pool(name="apool", bufs=2))
-        keep = ctx.enter_context(tc.tile_pool(name="keep", bufs=3))
-        psum = ctx.enter_context(tc.psum_pool(name="psum", bufs=2))
+        hpool = ctx.enter_context(tc.tile_pool(name="hpool", bufs=2))
+        keep = ctx.enter_context(tc.tile_pool(name="keep", bufs=AHEAD + 1))
+        tpool = ctx.enter_context(tc.tile_pool(name="tpool", bufs=3))
+        ps_t = ctx.enter_context(tc.psum_pool(name="ps_t", bufs=3))
+        ps_1 = ctx.enter_context(tc.psum_pool(name="ps_1", bufs=1))
+        ps_k = ctx.enter_context(tc.psum_pool(name="ps_k", bufs=3))
 
-        ident = const.tile([P, P], F32)
+        warm = const.tile([P, 1], F32, name="warm")
+        nc.vector.memset(warm[:], 0.0)
+        nc.scalar.activation(out=warm[:], in_=warm[:], func=ACT.Gelu_apprx_tanh)
+        ident = const.tile([P, P], F32, name="ident")
         make_identity(nc, ident[:])
-        bias_b = const.tile([P, C], BF16)
-        nc.sync.dma_start(out=bias_b[:], in_=b_skip.partition_broadcast(P))
-        bias4 = const.tile([P, C], F32)
-        nc.vector.tensor_scalar(out=bias4[:], in0=bias_b[:], scalar1=4.0, scalar2=None, op0=ALU.mult)
-
-        ws_codes = const.tile([P, C], U32, align_bytes=64)
-        ws_scales = const.tile([P, C], U8, align_bytes=64)
-        w_codes = []
-        w_scales = []
+        ident_b = const.tile([P, P], BF16, name="ident_b")
+        make_identity(nc, ident_b[:])
+        bias_b = const.tile([P, C], BF16, name="bias_b")
+        bias = const.tile([P, C], F32, name="bias")
+        ws_codes = const.tile([P, C], U32, align_bytes=64, name="ws_codes")
+        ws_scales = const.tile([P, C], U8, align_bytes=64, name="ws_scales")
+        w_codes = [[[None, None], [None, None]], [[None, None], [None, None]]]
+        w_scales = [[[None, None], [None, None]], [[None, None], [None, None]]]
         for s in range(2):
-            wc = const.tile([P, UNITS * C], U32, align_bytes=64, name="wc%d" % s)
-            wsc = const.tile([P, UNITS * C], U8, align_bytes=64, name="wsc%d" % s)
-            w_codes.append(wc)
-            w_scales.append(wsc)
+            for oh in range(2):
+                for lh in range(2):
+                    wc = const.tile([P, 1024], U32, align_bytes=64, name="wc%d%d%d" % (s, oh, lh))
+                    wsc = const.tile([P, 1024], U8, align_bytes=64, name="wsc%d%d%d" % (s, oh, lh))
+                    w_codes[s][oh][lh] = wc
+                    w_scales[s][oh][lh] = wsc
 
         xus = {}
+        state = {}
 
         def load_x(u):
             xu = xpool.tile([P, 8 * C], BF16, tag="xu", name="xu%d" % u)
             nc.sync.dma_start(out=xu[:], in_=x[:, 8 * u : 8 * u + 8, :].rearrange("b l c -> b (l c)"))
             xus[u] = xu
 
-        state = {}
-
-        def stage_a(u):
-            xu = xus[u]
-            xv = xu[:].rearrange("p (k two c) -> p k two c", two=2, c=C)
-            pp = ppool.tile([P, 4 * C], F32, tag="pp", name="pp%d" % u)
-            nc.gpsimd.tensor_tensor(
-                out=pp[:].rearrange("p (k c) -> p k c", c=C), in0=xv[:, :, 0, :], in1=xv[:, :, 1, :], op=ALU.add
-            )
-            pv = pp[:].rearrange("p (h two c) -> p h two c", two=2, c=C)
-            s4 = hpool.tile([P, 2 * C], F32, tag="s4", name="s4_%d" % u)
-            nc.gpsimd.tensor_tensor(
-                out=s4[:].rearrange("p (h c) -> p h c", c=C), in0=pv[:, :, 0, :], in1=pv[:, :, 1, :], op=ALU.add
-            )
-            ad = hpool.tile([P, 2 * C], F32, tag="ad", name="ad%d" % u)
-            nc.gpsimd.tensor_tensor(out=ad[:, 0:C], in0=s4[:, 0:C], in1=s4[:, C : 2 * C], op=ALU.add)
-            nc.gpsimd.tensor_tensor(out=ad[:, C : 2 * C], in0=s4[:, 0:C], in1=s4[:, C : 2 * C], op=ALU.subtract)
-            mm = keep.tile([P, 2 * C], F32, tag="mm", name="mm%d" % u)
-            nc.gpsimd.tensor_tensor(
-                out=mm[:].rearrange("p (h c) -> p h c", c=C),
-                in0=s4[:].rearrange("p (h c) -> p h c", c=C),
-                in1=bias4[:].unsqueeze(1).to_broadcast([P, 2, C]),
-                op=ALU.subtract,
-            )
-            xw = xu[:].bitcast(F32)
+        def pre_x(u, copies):
+            xw = xus[u][:].bitcast(F32)
             xg = gpool.tile([P, 8 * C], BF16, align_bytes=64, tag="xg", name="xg%d" % u)
             xgw = xg[:].bitcast(F32)
             for jp in range(4):
-                tin = psum.tile([P, C], F32, tag="tin", name="tin%d_%d" % (u, jp))
+                tin = ps_t.tile([P, C], F32, tag="tp", name="tin%d_%d" % (u, jp))
                 for jj in range(2):
                     j = 2 * jp + jj
                     for uu in range(2):
@@ -95,146 +76,214 @@ def tile_waveletblock1d_t_kernel(tc, x, w_approx, w_detail, W_skip, b_skip, out)
                             xw[:, j * 256 + uu : (j + 1) * 256 : 2],
                             ident[:],
                         )
-                nc.scalar.copy(
-                    out=xgw[:, jp * C : (jp + 1) * C].rearrange("p (n u) -> p n u", u=2),
-                    in_=tin[:].rearrange("p (u n) -> p n u", u=2),
-                )
-            x_codes = keep.tile([P, 8 * P], U32, align_bytes=64, tag="xc", name="xc%d" % u)
-            x_scales = keep.tile([P, 8 * P], U8, align_bytes=64, tag="xs", name="xs%d" % u)
-            nc.vector.quantize_mx(out=x_codes[:].bitcast(FP8X4), scales=x_scales[:], in_=xg[:])
-            gq = apool.tile([P, 3 * C], BF16, align_bytes=64, tag="gq", name="gq%d" % u)
+                dst = xgw[:, jp * C : (jp + 1) * C].rearrange("p (n u) -> p n u", u=2)
+                srcv = tin[:].rearrange("p (u n) -> p n u", u=2)
+                if copies[jp] == "v":
+                    nc.vector.tensor_copy(out=dst, in_=srcv)
+                else:
+                    nc.scalar.copy(out=dst, in_=srcv)
+            xc = keep.tile([P, 8 * P], U32, align_bytes=64, tag="xc", name="xc%d" % u)
+            xs = keep.tile([P, 8 * P], U8, align_bytes=64, tag="xs", name="xs%d" % u)
+            nc.vector.quantize_mx(out=xc[:].bitcast(FP8X4), scales=xs[:], in_=xg[:])
+            state[u] = [xc, xs]
+
+        def haar(u):
+            xu = xus[u]
+            s0 = ps_1.tile([P, C], F32, tag="s0", name="s0_%d" % u)
+            for j in range(4):
+                nc.tensor.matmul(s0[:], ident_b[:], xu[:, j * C : (j + 1) * C], start=(j == 0), stop=(j == 3))
+            xv = xu[:, 4 * C : 8 * C].rearrange("p (k two c) -> p k two c", two=2, c=C)
+            pp = hpool.tile([P, 2 * C], F32, tag="pp", name="pp%d" % u)
+            nc.gpsimd.tensor_tensor(
+                out=pp[:].rearrange("p (k c) -> p k c", c=C), in0=xv[:, :, 0, :], in1=xv[:, :, 1, :], op=ALU.add
+            )
+            s1 = hpool.tile([P, C], F32, tag="s1", name="s1_%d" % u)
+            nc.gpsimd.tensor_tensor(out=s1[:], in0=pp[:, 0:C], in1=pp[:, C : 2 * C], op=ALU.add)
+            n = keep.tile([P, 2 * C], F32, tag="n", name="n%d" % u)
+            nc.vector.scalar_tensor_tensor(
+                out=n[:, 0:C], in0=s0[:], scalar=-0.25, in1=bias[:], op0=ALU.mult, op1=ALU.add
+            )
+            ad = hpool.tile([P, 2 * C], F32, tag="ad", name="ad%d" % u)
+            s0v = s0[:].rearrange("p (q t) -> p t q", t=4)
+            s1v = s1[:].rearrange("p (q t) -> p t q", t=4)
             for s in range(2):
-                at = psum.tile([P, C], F32, tag="at", name="at%d_%d" % (u, s))
+                nc.vector.tensor_tensor(
+                    out=ad[:, s * C : (s + 1) * C].rearrange("p (t q) -> p t q", t=4),
+                    in0=s0v,
+                    in1=s1v,
+                    op=(ALU.add, ALU.subtract)[s],
+                )
+            nc.vector.scalar_tensor_tensor(
+                out=n[:, C : 2 * C], in0=s1[:], scalar=-0.25, in1=bias[:], op0=ALU.mult, op1=ALU.add
+            )
+            gq = hpool.tile([P, 3 * C], BF16, align_bytes=64, tag="gq", name="gq%d" % u)
+            for s in range(2):
+                at = ps_t.tile([P, C], F32, tag="tp", name="at%d_%d" % (u, s))
                 for t in range(4):
                     nc.tensor.transpose(
-                        at[:, t * P : (t + 1) * P], ad[:, s * C + t : (s + 1) * C : 4], ident[:]
+                        at[:, t * P : (t + 1) * P], ad[:, s * C + t * P : s * C + (t + 1) * P], ident[:]
                     )
-                av = at[:].rearrange("p (t b) -> p b t", t=4)
                 nc.scalar.activation(
-                    out=gq[:, s * C : (s + 1) * C].rearrange("p (b t) -> p b t", t=4), in_=av, func=ACT.Copy, scale=R3
+                    out=gq[:, s * C : (s + 1) * C].rearrange("p (b t) -> p b t", t=4),
+                    in_=at[:].rearrange("p (t b) -> p b t", t=4),
+                    func=ACT.Copy,
+                    scale=R3,
                 )
-                if s == 1:
-                    nc.scalar.activation(
-                        out=gq[:, 2 * C : 3 * C].rearrange("p (b t) -> p b t", t=4), in_=av, func=ACT.Copy, scale=-R3
-                    )
-            a_codes = keep.tile([P, 3 * P], U32, align_bytes=64, tag="ac", name="ac%d" % u)
-            a_scales = keep.tile([P, 3 * P], U8, align_bytes=64, tag="as", name="as%d" % u)
-            nc.vector.quantize_mx(
-                out=a_codes[:, 0 : 2 * P].bitcast(FP8X4), scales=a_scales[:, 0 : 2 * P], in_=gq[:, 0 : 2 * C]
+            nc.vector.tensor_scalar(
+                out=gq[:, 2 * C : 3 * C], in0=gq[:, C : 2 * C], scalar1=-1.0, scalar2=None, op0=ALU.mult
             )
+            ac = keep.tile([P, 3 * P], U32, align_bytes=64, tag="ac", name="ac%d" % u)
+            asc = keep.tile([P, 3 * P], U8, align_bytes=64, tag="as", name="as%d" % u)
+            nc.vector.quantize_mx(out=ac[:, 0 : 2 * P].bitcast(FP8X4), scales=asc[:, 0 : 2 * P], in_=gq[:, 0 : 2 * C])
             nc.vector.quantize_mx(
-                out=a_codes[:, 2 * P : 3 * P].bitcast(FP8X4), scales=a_scales[:, 2 * P : 3 * P], in_=gq[:, 2 * C : 3 * C]
+                out=ac[:, 2 * P : 3 * P].bitcast(FP8X4), scales=asc[:, 2 * P : 3 * P], in_=gq[:, 2 * C : 3 * C]
             )
-            state[u] = (mm, x_codes, x_scales, a_codes, a_scales)
+            state[u] += [ac, asc, n]
 
-        wsraw = xpool.tile([P, 8 * C], BF16, tag="xu", name="wsraw")
-        nc.sync.dma_start(
-            out=wsraw[:, 0 : 4 * C].rearrange("p (u r) -> p u r", u=2),
-            in_=W_skip.rearrange("(q u e) o -> q u (e o)", u=2, e=2),
-        )
-        load_x(0)
-        with tc.tile_pool(name="wstage", bufs=2) as wstage:
-            wsg = wstage.tile([P, 8 * OC * 4], BF16, align_bytes=64, tag="wg", name="wsg")
+        def skip(u, j):
+            sk = ps_k.tile([P, C], F32, tag="sk", name="sk%d_%d" % (u, j))
+            xc, xs = state[u][0:2]
+            nc.tensor.matmul_mx(
+                out=sk[:],
+                lhsT=xc[:, j * P : (j + 1) * P].bitcast(FP8X4),
+                lhsT_scale=xs[:, j * P : (j + 1) * P],
+                rhs=ws_codes[:].bitcast(FP8X4),
+                rhs_scale=ws_scales[:],
+                start=True,
+                stop=True,
+            )
+            return sk
+
+        def early(u, h):
+            tt = tpool.tile([P, 4 * C], F32, tag="t", name="t%d_%d" % (u, h))
+            for jj in range(4):
+                j = 4 * h + jj
+                sk = skip(u, j)
+                nc.vector.tensor_tensor(
+                    out=tt[:, jj * C : (jj + 1) * C], in0=sk[:], in1=xus[u][:, j * C : (j + 1) * C], op=ALU.add
+                )
+            return tt
+
+        def wide(ap):
+            return ap.unsqueeze(1).to_broadcast([P, 4, C])
+
+        def finish(u, h, z):
+            nc.scalar.activation(out=z[:], in_=z[:], func=ACT.Gelu_apprx_tanh)
+            nc.sync.dma_start(out=out[:, 8 * u + 4 * h : 8 * u + 4 * h + 4, :].rearrange("b l o -> b (l o)"), in_=z[:])
+
+        with tc.tile_pool(name="wstage", bufs=2) as wstage, tc.tile_pool(name="wraw", bufs=3) as rawpool:
+
+            def load_w(s, oq):
+                w = (w_approx, w_detail)[s]
+                raw = rawpool.tile([P, 4 * P * 8], BF16, tag="raw", name="raw%d_%d" % (s, oq))
+                nc.sync.dma_start(
+                    out=raw[:].rearrange("p (t r) -> p t r", t=4),
+                    in_=w.rearrange("(p t) o l -> p t o l", t=4)[:, :, oq * P : (oq + 1) * P, :].rearrange(
+                        "p t o l -> p t (o l)"
+                    ),
+                )
+                return raw
+
+            raws = {(0, 0): load_w(0, 0)}
+            wsraw = gpool.tile([P, 8 * C], BF16, align_bytes=64, tag="xg", name="wsraw")
+            nc.sync.dma_start(
+                out=wsraw[:, 0 : 4 * C].rearrange("p (t o) -> p t o", t=4),
+                in_=W_skip.rearrange("(q t) o -> q t o", t=4),
+            )
+            load_x(0)
+            raws[(0, 1)] = load_w(0, 1)
+            nc.sync.dma_start(out=bias_b[:], in_=b_skip.partition_broadcast(P))
+            nc.vector.tensor_copy(out=bias[:], in_=bias_b[:])
+
+            wsg = wsraw[:, 4 * C : 8 * C]
             nc.vector.tensor_copy(
-                out=wsg[:, 0 : 4 * C].rearrange("p (o t) -> p o t", t=4),
+                out=wsg.rearrange("p (o t) -> p o t", t=4),
                 in_=wsraw[:, 0 : 4 * C].rearrange("p (t o) -> p o t", t=4),
             )
-            nc.vector.quantize_mx(out=ws_codes[:].bitcast(FP8X4), scales=ws_scales[:], in_=wsg[:, 0 : 4 * C])
-            raws = []
-            for s, w in enumerate((w_approx, w_detail)):
-                wv = w.rearrange("(p t) o l -> p t o l", t=4)
-                for ch in range(C // OC):
-                    wraw = wstage.tile([P, 4 * OC * 8], BF16, tag="wraw", name="wraw%d_%d" % (s, ch))
-                    nc.sync.dma_start(
-                        out=wraw[:].rearrange("p (t r) -> p t r", t=4),
-                        in_=wv[:, :, ch * OC : (ch + 1) * OC, :].rearrange("p t o l -> p t (o l)"),
-                    )
-                    raws.append((s, ch, wraw))
-                    if ch == 1:
-                        load_x(1 + s)
-            stage_a(0)
-            for s, ch, wraw in raws:
-                wg = wstage.tile([P, 8 * OC * 4], BF16, align_bytes=64, tag="wg", name="wg%d_%d" % (s, ch))
-                src = wraw[:].rearrange("p (t o l) -> p l o t", t=4, l=8)
-                dst = wg[:].rearrange("p (l o t) -> p l o t", l=8, t=4)
-                nc.vector.tensor_copy(out=dst[:, 0:4], in_=src[:, 0:4])
-                nc.scalar.copy(out=dst[:, 5:8], in_=src[:, 5:8])
-                nc.vector.tensor_copy(out=dst[:, 4], in_=src[:, 4])
-                for l in range(8):
+            nc.vector.quantize_mx(out=ws_codes[:].bitcast(FP8X4), scales=ws_scales[:], in_=wsg)
+
+            tts = {}
+            for g in range(4):
+                s, oh = divmod(g, 2)
+                for oq in (2 * oh, 2 * oh + 1):
+                    if (s, oq) not in raws:
+                        raws[(s, oq)] = load_w(s, oq)
+                if g < 3:
+                    load_x(g + 1)
+                for lh in range(2):
+                    wg = wstage.tile([P, 4096], BF16, align_bytes=64, tag="wg", name="wg%d_%d" % (g, lh))
+                    for i in range(2):
+                        raw = raws[(s, 2 * oh + i)]
+                        srcv = raw[:].rearrange("p (t o l) -> p l o t", t=4, l=8)[:, 4 * lh : 4 * lh + 4]
+                        dstv = wg[:].rearrange("p (l o t) -> p l o t", l=4, t=4)[:, :, i * P : (i + 1) * P, :]
+                        if lh == 1 and i == 1:
+                            nc.vector.tensor_copy(out=dstv, in_=srcv)
+                        else:
+                            nc.scalar.copy(out=dstv, in_=srcv)
                     nc.vector.quantize_mx(
-                        out=w_codes[s][:, l * C + ch * OC : l * C + (ch + 1) * OC].bitcast(FP8X4),
-                        scales=w_scales[s][:, l * C + ch * OC : l * C + (ch + 1) * OC],
-                        in_=wg[:, l * OC * 4 : (l + 1) * OC * 4],
+                        out=w_codes[s][oh][lh][:].bitcast(FP8X4), scales=w_scales[s][oh][lh][:], in_=wg[:]
                     )
-                if ch == 1:
-                    stage_a(1 + s)
+                if g < 3:
+                    pre_x(g, "vvvv")
+                    haar(g)
+                    tts[(g, 0)] = early(g, 0)
 
         zpool = ctx.enter_context(tc.tile_pool(name="zpool", bufs=4))
 
-        def stage_b(u):
+        def post(u):
             xu = xus[u]
-            mm, x_codes, x_scales, a_codes, a_scales = state[u]
+            ac, asc, n = state[u][2:5]
             cc = hpool.tile([P, 2 * C], F32, tag="cc", name="cc%d" % u)
+            lh, li = divmod(u, 4)
+            cols = slice(li * 256, (li + 1) * 256)
             for h in range(2):
-                mx = psum.tile([P, C], F32, tag="mix", name="mix%d_%d" % (u, h))
-                nc.tensor.matmul_mx(
-                    out=mx[:],
-                    lhsT=a_codes[:, 0:P].bitcast(FP8X4),
-                    lhsT_scale=a_scales[:, 0:P],
-                    rhs=w_codes[0][:, u * C : (u + 1) * C].bitcast(FP8X4),
-                    rhs_scale=w_scales[0][:, u * C : (u + 1) * C],
-                    start=True,
-                    stop=False,
-                )
-                nc.tensor.matmul_mx(
-                    out=mx[:],
-                    lhsT=a_codes[:, (1 + h) * P : (2 + h) * P].bitcast(FP8X4),
-                    lhsT_scale=a_scales[:, (1 + h) * P : (2 + h) * P],
-                    rhs=w_codes[1][:, u * C : (u + 1) * C].bitcast(FP8X4),
-                    rhs_scale=w_scales[1][:, u * C : (u + 1) * C],
-                    start=False,
-                    stop=True,
-                )
+                mx = ps_1.tile([P, C], F32, tag="mix", name="mix%d_%d" % (u, h))
+                for oh in range(2):
+                    for s in range(2):
+                        a0 = (0, 1 + h)[s] * P
+                        nc.tensor.matmul_mx(
+                            out=mx[:, oh * 256 : (oh + 1) * 256],
+                            lhsT=ac[:, a0 : a0 + P].bitcast(FP8X4),
+                            lhsT_scale=asc[:, a0 : a0 + P],
+                            rhs=w_codes[s][oh][lh][:, cols].bitcast(FP8X4),
+                            rhs_scale=w_scales[s][oh][lh][:, cols],
+                            start=(s == 0),
+                            stop=(s == 1),
+                        )
                 nc.vector.scalar_tensor_tensor(
                     out=cc[:, h * C : (h + 1) * C],
                     in0=mx[:],
-                    scalar=-4.0 * R3,
-                    in1=mm[:, h * C : (h + 1) * C],
+                    scalar=R3,
+                    in1=n[:, h * C : (h + 1) * C],
                     op0=ALU.mult,
                     op1=ALU.add,
                 )
-                z = zpool.tile([P, 4 * C], F32, tag="z", name="z%d_%d" % (u, h))
-                nc.vector.scalar_tensor_tensor(
-                    out=z[:].rearrange("p (j c) -> p j c", c=C),
-                    in0=cc[:, h * C : (h + 1) * C].unsqueeze(1).to_broadcast([P, 4, C]),
-                    scalar=-0.25,
-                    in1=xu[:, h * 4 * C : (h + 1) * 4 * C].rearrange("p (j c) -> p j c", c=C),
-                    op0=ALU.mult,
-                    op1=ALU.add,
+            z = zpool.tile([P, 4 * C], F32, tag="z", name="z%d" % u)
+            nc.gpsimd.tensor_tensor(
+                out=z[:].rearrange("p (j c) -> p j c", c=C),
+                in0=xu[:, 4 * C : 8 * C].rearrange("p (j c) -> p j c", c=C),
+                in1=wide(cc[:, C : 2 * C]),
+                op=ALU.add,
+            )
+            tt = tts[(u, 0)] if (u, 0) in tts else early(u, 0)
+            nc.vector.tensor_tensor(
+                out=tt[:].rearrange("p (j c) -> p j c", c=C),
+                in0=tt[:].rearrange("p (j c) -> p j c", c=C),
+                in1=wide(cc[:, 0:C]),
+                op=ALU.add,
+            )
+            finish(u, 0, tt)
+            for jj in range(4):
+                sk = skip(u, 4 + jj)
+                nc.vector.tensor_tensor(
+                    out=z[:, jj * C : (jj + 1) * C], in0=sk[:], in1=z[:, jj * C : (jj + 1) * C], op=ALU.add
                 )
-                for jj in range(4):
-                    j = 4 * h + jj
-                    sk = psum.tile([P, C], F32, tag="sk", name="sk%d_%d" % (u, j))
-                    nc.tensor.matmul_mx(
-                        out=sk[:],
-                        lhsT=x_codes[:, j * P : (j + 1) * P].bitcast(FP8X4),
-                        lhsT_scale=x_scales[:, j * P : (j + 1) * P],
-                        rhs=ws_codes[:].bitcast(FP8X4),
-                        rhs_scale=ws_scales[:],
-                        start=True,
-                        stop=True,
-                    )
-                    nc.vector.tensor_tensor(
-                        out=z[:, jj * C : (jj + 1) * C], in0=sk[:], in1=z[:, jj * C : (jj + 1) * C], op=ALU.add
-                    )
-                nc.scalar.activation(out=z[:], in_=z[:], func=ACT.Gelu_apprx_tanh)
-                nc.scalar.dma_start(
-                    out=out[:, 8 * u + 4 * h : 8 * u + 4 * h + 4, :].rearrange("b l o -> b (l o)"), in_=z[:]
-                )
+            finish(u, 1, z)
 
         for u in range(UNITS):
-            if u + 3 < UNITS:
-                load_x(u + 3)
-            stage_b(u)
-            if u + 3 < UNITS:
-                stage_a(u + 3)
+            if u + AHEAD < UNITS:
+                if u > 0:
+                    load_x(u + AHEAD)
+                pre_x(u + AHEAD, "ssss")
+                haar(u + AHEAD)
+            post(u)

@@ -104,11 +104,11 @@ def tile_waveletblock1d_t_kernel(tc, x, w_approx, w_detail, W_skip, b_skip, out)
                 out=n[:, 0:C], in0=s0[:], scalar=-0.25, in1=bias[:], op0=ALU.mult, op1=ALU.add
             )
             ad = hpool.tile([P, 2 * C], F32, tag="ad", name="ad%d" % u)
-            s0v = s0[:].rearrange("p (q t) -> p t q", t=4)
-            s1v = s1[:].rearrange("p (q t) -> p t q", t=4)
+            s0v = s0[:].rearrange("p (q t) -> p q t", t=4)
+            s1v = s1[:].rearrange("p (q t) -> p q t", t=4)
             for s in range(2):
                 nc.vector.tensor_tensor(
-                    out=ad[:, s * C : (s + 1) * C].rearrange("p (t q) -> p t q", t=4),
+                    out=ad[:, s * C : (s + 1) * C].rearrange("p (t q) -> p q t", t=4),
                     in0=s0v,
                     in1=s1v,
                     op=(ALU.add, ALU.subtract)[s],
@@ -214,8 +214,8 @@ def tile_waveletblock1d_t_kernel(tc, x, w_approx, w_detail, W_skip, b_skip, out)
                     wg = wstage.tile([P, 4096], BF16, align_bytes=64, tag="wg", name="wg%d_%d" % (g, lh))
                     for i in range(2):
                         raw = raws[(s, 2 * oh + i)]
-                        srcv = raw[:].rearrange("p (t o l) -> p l o t", t=4, l=8)[:, 4 * lh : 4 * lh + 4]
-                        dstv = wg[:].rearrange("p (l o t) -> p l o t", l=4, t=4)[:, :, i * P : (i + 1) * P, :]
+                        srcv = raw[:].rearrange("p (t o l) -> p o l t", t=4, l=8)[:, :, 4 * lh : 4 * lh + 4]
+                        dstv = wg[:].rearrange("p (l o t) -> p o l t", l=4, t=4)[:, i * P : (i + 1) * P]
                         if lh == 1 and i == 1:
                             nc.vector.tensor_copy(out=dstv, in_=srcv)
                         else:

@@ -17,21 +17,20 @@ UNITS = 8
 R = 0.7071067811865476
 R3 = R * R * R
 FLOPS = 2 * 8192 * 512 * 512 + 2 * 2 * 8 * 128 * 512 * 512
-AHEAD = 3
 
 
 def tile_waveletblock1d_t_kernel(tc, x, w_approx, w_detail, W_skip, b_skip, out):
     nc = tc.nc
     with ExitStack() as ctx:
+        ctx.enter_context(tc.manual_schedule())
         const = ctx.enter_context(tc.tile_pool(name="const", bufs=1))
-        xpool = ctx.enter_context(tc.tile_pool(name="xpool", bufs=AHEAD + 1))
-        gpool = ctx.enter_context(tc.tile_pool(name="gpool", bufs=2))
-        hpool = ctx.enter_context(tc.tile_pool(name="hpool", bufs=2))
-        keep = ctx.enter_context(tc.tile_pool(name="keep", bufs=AHEAD + 1))
-        tpool = ctx.enter_context(tc.tile_pool(name="tpool", bufs=3))
-        ps_t = ctx.enter_context(tc.psum_pool(name="ps_t", bufs=3))
+        pool1 = ctx.enter_context(tc.tile_pool(name="pool1", bufs=1))
+        pool2 = ctx.enter_context(tc.tile_pool(name="pool2", bufs=2))
+        pool3 = ctx.enter_context(tc.tile_pool(name="pool3", bufs=3))
+        pool4 = ctx.enter_context(tc.tile_pool(name="pool4", bufs=4))
+        xpool = ctx.enter_context(tc.tile_pool(name="xpool", bufs=5))
+        ps_2 = ctx.enter_context(tc.psum_pool(name="ps_2", bufs=2))
         ps_1 = ctx.enter_context(tc.psum_pool(name="ps_1", bufs=1))
-        ps_k = ctx.enter_context(tc.psum_pool(name="ps_k", bufs=3))
 
         warm = const.tile([P, 1], F32, name="warm")
         nc.vector.memset(warm[:], 0.0)
@@ -41,7 +40,7 @@ def tile_waveletblock1d_t_kernel(tc, x, w_approx, w_detail, W_skip, b_skip, out)
         ident_b = const.tile([P, P], BF16, name="ident_b")
         make_identity(nc, ident_b[:])
         bias_b = const.tile([P, C], BF16, name="bias_b")
-        bias = const.tile([P, C], F32, name="bias")
+        bias_t = const.tile([P, C], F32, name="bias_t")
         ws_codes = const.tile([P, C], U32, align_bytes=64, name="ws_codes")
         ws_scales = const.tile([P, C], U8, align_bytes=64, name="ws_scales")
         w_codes = [[[None, None], [None, None]], [[None, None], [None, None]]]
@@ -55,94 +54,151 @@ def tile_waveletblock1d_t_kernel(tc, x, w_approx, w_detail, W_skip, b_skip, out)
                     w_scales[s][oh][lh] = wsc
 
         xus = {}
-        state = {}
+        xgs = {}
+        xqs = {}
+        s0ps = {}
+        s0s = {}
+        s1s = {}
+        aqs = {}
+        cts = {}
+        cps = {}
+        zs = {}
 
         def load_x(u):
             xu = xpool.tile([P, 8 * C], BF16, tag="xu", name="xu%d" % u)
             nc.sync.dma_start(out=xu[:], in_=x[:, 8 * u : 8 * u + 8, :].rearrange("b l c -> b (l c)"))
             xus[u] = xu
 
-        def pre_x(u, copies):
+        def turn_x(u, jp, engine):
+            if jp == 0:
+                xg = pool2.tile([P, 8 * C], BF16, align_bytes=64, tag="xg", name="xg%d" % u)
+                xgs[u] = xg
             xw = xus[u][:].bitcast(F32)
-            xg = gpool.tile([P, 8 * C], BF16, align_bytes=64, tag="xg", name="xg%d" % u)
-            xgw = xg[:].bitcast(F32)
-            for jp in range(4):
-                tin = ps_t.tile([P, C], F32, tag="tp", name="tin%d_%d" % (u, jp))
-                for jj in range(2):
-                    j = 2 * jp + jj
-                    for uu in range(2):
-                        nc.tensor.transpose(
-                            tin[:, uu * 256 + jj * P : uu * 256 + jj * P + P],
-                            xw[:, j * 256 + uu : (j + 1) * 256 : 2],
-                            ident[:],
-                        )
-                dst = xgw[:, jp * C : (jp + 1) * C].rearrange("p (n u) -> p n u", u=2)
-                srcv = tin[:].rearrange("p (u n) -> p n u", u=2)
-                if copies[jp] == "v":
-                    nc.vector.tensor_copy(out=dst, in_=srcv)
-                else:
-                    nc.scalar.copy(out=dst, in_=srcv)
-            xc = keep.tile([P, 8 * P], U32, align_bytes=64, tag="xc", name="xc%d" % u)
-            xs = keep.tile([P, 8 * P], U8, align_bytes=64, tag="xs", name="xs%d" % u)
-            nc.vector.quantize_mx(out=xc[:].bitcast(FP8X4), scales=xs[:], in_=xg[:])
-            state[u] = [xc, xs]
-
-        def haar(u):
-            xu = xus[u]
-            s0 = ps_1.tile([P, C], F32, tag="s0", name="s0_%d" % u)
-            for j in range(4):
-                nc.tensor.matmul(s0[:], ident_b[:], xu[:, j * C : (j + 1) * C], start=(j == 0), stop=(j == 3))
-            xv = xu[:, 4 * C : 8 * C].rearrange("p (k two c) -> p k two c", two=2, c=C)
-            pp = hpool.tile([P, 2 * C], F32, tag="pp", name="pp%d" % u)
-            nc.gpsimd.tensor_tensor(
-                out=pp[:].rearrange("p (k c) -> p k c", c=C), in0=xv[:, :, 0, :], in1=xv[:, :, 1, :], op=ALU.add
-            )
-            s1 = hpool.tile([P, C], F32, tag="s1", name="s1_%d" % u)
-            nc.gpsimd.tensor_tensor(out=s1[:], in0=pp[:, 0:C], in1=pp[:, C : 2 * C], op=ALU.add)
-            n = keep.tile([P, 2 * C], F32, tag="n", name="n%d" % u)
-            nc.vector.scalar_tensor_tensor(
-                out=n[:, 0:C], in0=s0[:], scalar=-0.25, in1=bias[:], op0=ALU.mult, op1=ALU.add
-            )
-            ad = hpool.tile([P, 2 * C], F32, tag="ad", name="ad%d" % u)
-            s0v = s0[:].rearrange("p (q t) -> p q t", t=4)
-            s1v = s1[:].rearrange("p (q t) -> p q t", t=4)
-            for s in range(2):
-                nc.vector.tensor_tensor(
-                    out=ad[:, s * C : (s + 1) * C].rearrange("p (t q) -> p q t", t=4),
-                    in0=s0v,
-                    in1=s1v,
-                    op=(ALU.add, ALU.subtract)[s],
-                )
-            nc.vector.scalar_tensor_tensor(
-                out=n[:, C : 2 * C], in0=s1[:], scalar=-0.25, in1=bias[:], op0=ALU.mult, op1=ALU.add
-            )
-            gq = hpool.tile([P, 3 * C], BF16, align_bytes=64, tag="gq", name="gq%d" % u)
-            for s in range(2):
-                at = ps_t.tile([P, C], F32, tag="tp", name="at%d_%d" % (u, s))
-                for t in range(4):
+            tin = ps_2.tile([P, C], F32, tag="tin", name="tin%d_%d" % (u, jp))
+            for jj in range(2):
+                j = 2 * jp + jj
+                for uu in range(2):
                     nc.tensor.transpose(
-                        at[:, t * P : (t + 1) * P], ad[:, s * C + t * P : s * C + (t + 1) * P], ident[:]
+                        tin[:, uu * 256 + jj * P : uu * 256 + jj * P + P],
+                        xw[:, j * 256 + uu : (j + 1) * 256 : 2],
+                        ident[:],
                     )
-                nc.scalar.activation(
+            dst = xgs[u][:].bitcast(F32)[:, jp * C : (jp + 1) * C].rearrange("p (n u) -> p n u", u=2)
+            srcv = tin[:].rearrange("p (u n) -> p n u", u=2)
+            if engine == "v":
+                nc.vector.tensor_copy(out=dst, in_=srcv)
+            else:
+                nc.scalar.copy(out=dst, in_=srcv)
+
+        def quant_x(u):
+            xc = pool4.tile([P, 8 * P], U32, align_bytes=64, tag="xc", name="xc%d" % u)
+            xs = pool4.tile([P, 8 * P], U8, align_bytes=64, tag="xs", name="xs%d" % u)
+            nc.vector.quantize_mx(out=xc[:].bitcast(FP8X4), scales=xs[:], in_=xgs[u][:])
+            xqs[u] = (xc, xs)
+
+        def sum0(u):
+            s0p = ps_1.tile([P, C], F32, tag="s0p", name="s0p%d" % u)
+            for t in range(4):
+                for j in range(4):
+                    nc.tensor.matmul(
+                        s0p[:, t * P : (t + 1) * P],
+                        xus[u][:, j * C + t : (j + 1) * C : 4],
+                        ident_b[:],
+                        start=(j == 0),
+                        stop=(j == 3),
+                    )
+            s0ps[u] = s0p
+
+        def keep0(u):
+            s0 = pool2.tile([P, C], F32, tag="s0", name="s0_%d" % u)
+            nc.scalar.copy(out=s0[:], in_=s0ps[u][:])
+            s0s[u] = s0
+
+        def sum1(u):
+            xv = xgs[u][:, 4 * C : 8 * C].rearrange("p (k two b t) -> p k two t b", two=2, b=P, t=4)
+            pp = pool1.tile([P, 2 * C], F32, tag="pp", name="pp%d" % u)
+            for k in range(2):
+                nc.gpsimd.tensor_tensor(
+                    out=pp[:, k * C : (k + 1) * C].rearrange("p (t b) -> p t b", t=4),
+                    in0=xv[:, k, 0],
+                    in1=xv[:, k, 1],
+                    op=ALU.add,
+                )
+            s1 = pool2.tile([P, C], F32, tag="s1", name="s1_%d" % u)
+            nc.gpsimd.tensor_tensor(out=s1[:], in0=pp[:, 0:C], in1=pp[:, C : 2 * C], op=ALU.add)
+            s1s[u] = s1
+
+        def make_a(u):
+            s1r = pool1.tile([P, C], F32, tag="s1r", name="s1r%d" % u)
+            nc.vector.tensor_scalar(out=s1r[:], in0=s1s[u][:], scalar1=R3, scalar2=None, op0=ALU.mult)
+            gq = pool2.tile([P, 3 * C], BF16, align_bytes=64, tag="gq", name="gq%d" % u)
+            for s in (1, 0):
+                nc.vector.scalar_tensor_tensor(
                     out=gq[:, s * C : (s + 1) * C].rearrange("p (b t) -> p b t", t=4),
-                    in_=at[:].rearrange("p (t b) -> p b t", t=4),
-                    func=ACT.Copy,
-                    scale=R3,
+                    in0=s0ps[u][:].rearrange("p (t b) -> p b t", t=4),
+                    scalar=R3,
+                    in1=s1r[:].rearrange("p (t b) -> p b t", t=4),
+                    op0=ALU.mult,
+                    op1=(ALU.add, ALU.subtract)[s],
                 )
             nc.vector.tensor_scalar(
                 out=gq[:, 2 * C : 3 * C], in0=gq[:, C : 2 * C], scalar1=-1.0, scalar2=None, op0=ALU.mult
             )
-            ac = keep.tile([P, 3 * P], U32, align_bytes=64, tag="ac", name="ac%d" % u)
-            asc = keep.tile([P, 3 * P], U8, align_bytes=64, tag="as", name="as%d" % u)
+            ac = pool2.tile([P, 3 * P], U32, align_bytes=64, tag="ac", name="ac%d" % u)
+            asc = pool2.tile([P, 3 * P], U8, align_bytes=64, tag="as", name="as%d" % u)
             nc.vector.quantize_mx(out=ac[:, 0 : 2 * P].bitcast(FP8X4), scales=asc[:, 0 : 2 * P], in_=gq[:, 0 : 2 * C])
             nc.vector.quantize_mx(
                 out=ac[:, 2 * P : 3 * P].bitcast(FP8X4), scales=asc[:, 2 * P : 3 * P], in_=gq[:, 2 * C : 3 * C]
             )
-            state[u] += [ac, asc, n]
+            aqs[u] = (ac, asc)
+
+        def mix(u, h):
+            ac, asc = aqs[u]
+            lh, li = divmod(u, 4)
+            mx = ps_1.tile([P, C], F32, tag="mix", name="mix%d_%d" % (u, h))
+            for ob in range(4):
+                w0 = li * 256 + (ob % 2) * P
+                for s in range(2):
+                    a0 = (0, 1 + h)[s] * P
+                    nc.tensor.matmul_mx(
+                        out=mx[:, ob * P : (ob + 1) * P],
+                        lhsT=w_codes[s][ob // 2][lh][:, w0 : w0 + P].bitcast(FP8X4),
+                        lhsT_scale=w_scales[s][ob // 2][lh][:, w0 : w0 + P],
+                        rhs=ac[:, a0 : a0 + P].bitcast(FP8X4),
+                        rhs_scale=asc[:, a0 : a0 + P],
+                        start=(s == 0),
+                        stop=(s == 1),
+                    )
+            ct = pool2.tile([P, C], F32, tag="ct", name="ct%d_%d" % (u, h))
+            nc.scalar.mul(ct[:], mx[:], -4.0 * R3)
+            cts[u, h] = ct
+
+        def coarse(u, h):
+            cp = ps_2.tile([P, C], F32, tag="cp", name="cp%d_%d" % (u, h))
+            for i, part in enumerate((bias_t, cts[u, h])):
+                for ob in range(4):
+                    nc.tensor.matmul(
+                        cp[:, ob * P : (ob + 1) * P],
+                        part[:, ob * P : (ob + 1) * P],
+                        ident[:],
+                        start=(i == 0 and ob == 0),
+                        stop=False,
+                        is_transpose=True,
+                    )
+            for t in range(4):
+                nc.tensor.matmul(
+                    cp[:, t : C : 4],
+                    (s0s, s1s)[h][u][:, t * P : (t + 1) * P],
+                    ident[:],
+                    start=False,
+                    stop=(t == 3),
+                    is_transpose=True,
+                )
+            cps[u, h] = cp
 
         def skip(u, j):
-            sk = ps_k.tile([P, C], F32, tag="sk", name="sk%d_%d" % (u, j))
-            xc, xs = state[u][0:2]
+            sk = ps_2.tile([P, C], F32, tag="sk", name="sk%d_%d" % (u, j))
+            xc, xs = xqs[u]
             nc.tensor.matmul_mx(
                 out=sk[:],
                 lhsT=xc[:, j * P : (j + 1) * P].bitcast(FP8X4),
@@ -155,45 +211,93 @@ def tile_waveletblock1d_t_kernel(tc, x, w_approx, w_detail, W_skip, b_skip, out)
             return sk
 
         def early(u, h):
-            tt = tpool.tile([P, 4 * C], F32, tag="t", name="t%d_%d" % (u, h))
+            tt = pool3.tile([P, 4 * C], F32, tag="t", name="t%d_%d" % (u, h))
             for jj in range(4):
                 j = 4 * h + jj
                 sk = skip(u, j)
                 nc.vector.tensor_tensor(
                     out=tt[:, jj * C : (jj + 1) * C], in0=sk[:], in1=xus[u][:, j * C : (j + 1) * C], op=ALU.add
                 )
-            return tt
+            zs[u, h] = tt
 
         def wide(ap):
             return ap.unsqueeze(1).to_broadcast([P, 4, C])
 
-        def finish(u, h, z):
+        def add_coarse(u, h):
+            z4 = zs[u, h][:].rearrange("p (j c) -> p j c", c=C)
+            nc.vector.scalar_tensor_tensor(
+                out=z4, in0=wide(cps[u, h][:]), scalar=-0.25, in1=z4, op0=ALU.mult, op1=ALU.add
+            )
+
+        def pool_add(u, h):
+            cc = pool2.tile([P, C], F32, tag="cc", name="cc%d" % u)
+            nc.scalar.mul(cc[:], cps[u, h][:], -0.25)
+            z = zpool.tile([P, 4 * C], F32, tag="z", name="z%d" % u)
+            nc.gpsimd.tensor_tensor(
+                out=z[:].rearrange("p (j c) -> p j c", c=C),
+                in0=xus[u][:, 4 * h * C : 4 * (h + 1) * C].rearrange("p (j c) -> p j c", c=C),
+                in1=wide(cc[:]),
+                op=ALU.add,
+            )
+            zs[u, h] = z
+
+        def add_skip(u, h):
+            z = zs[u, h]
+            for jj in range(4):
+                sk = skip(u, 4 * h + jj)
+                nc.vector.tensor_tensor(
+                    out=z[:, jj * C : (jj + 1) * C], in0=sk[:], in1=z[:, jj * C : (jj + 1) * C], op=ALU.add
+                )
+
+        def finish(u, h):
+            z = zs[u, h]
             nc.scalar.activation(out=z[:], in_=z[:], func=ACT.Gelu_apprx_tanh)
             nc.sync.dma_start(out=out[:, 8 * u + 4 * h : 8 * u + 4 * h + 4, :].rearrange("b l o -> b (l o)"), in_=z[:])
 
         with tc.tile_pool(name="wstage", bufs=2) as wstage, tc.tile_pool(name="wraw", bufs=3) as rawpool:
+            raws = {}
+            wgs = {}
 
-            def load_w(s, oq):
-                w = (w_approx, w_detail)[s]
-                raw = rawpool.tile([P, 4 * P * 8], BF16, tag="raw", name="raw%d_%d" % (s, oq))
+            def load_w(g, i):
+                s, oh = divmod(g, 2)
+                oq = 2 * oh + i
+                raw = rawpool.tile([P, 4 * P * 8], BF16, tag="raw", name="raw%d_%d" % (g, i))
                 nc.sync.dma_start(
                     out=raw[:].rearrange("p (t r) -> p t r", t=4),
-                    in_=w.rearrange("(p t) o l -> p t o l", t=4)[:, :, oq * P : (oq + 1) * P, :].rearrange(
-                        "p t o l -> p t (o l)"
-                    ),
+                    in_=(w_approx, w_detail)[s]
+                    .rearrange("(p t) o l -> p t o l", t=4)[:, :, oq * P : (oq + 1) * P, :]
+                    .rearrange("p t o l -> p t (o l)"),
                 )
-                return raw
+                raws[g, i] = raw
 
-            raws = {(0, 0): load_w(0, 0)}
-            wsraw = gpool.tile([P, 8 * C], BF16, align_bytes=64, tag="xg", name="wsraw")
+            def lay_w(g, i, lh, engine):
+                if i == 0:
+                    wg = wstage.tile([P, 4096], BF16, align_bytes=64, tag="wg", name="wg%d_%d" % (g, lh))
+                    wgs[g, lh] = wg
+                srcv = raws[g, i][:].rearrange("p (t o l) -> p o l t", t=4, l=8)[:, :, 4 * lh : 4 * lh + 4]
+                dstv = wgs[g, lh][:].rearrange("p (l o t) -> p o l t", l=4, t=4)[:, i * P : (i + 1) * P]
+                if engine == "v":
+                    nc.vector.tensor_copy(out=dstv, in_=srcv)
+                else:
+                    nc.scalar.copy(out=dstv, in_=srcv)
+
+            def quant_w(g, lh):
+                s, oh = divmod(g, 2)
+                nc.vector.quantize_mx(
+                    out=w_codes[s][oh][lh][:].bitcast(FP8X4), scales=w_scales[s][oh][lh][:], in_=wgs[g, lh][:]
+                )
+
+            load_w(0, 0)
+            wsraw = pool2.tile([P, 8 * C], BF16, align_bytes=64, tag="xg", name="wsraw")
             nc.sync.dma_start(
                 out=wsraw[:, 0 : 4 * C].rearrange("p (t o) -> p t o", t=4),
                 in_=W_skip.rearrange("(q t) o -> q t o", t=4),
             )
             load_x(0)
-            raws[(0, 1)] = load_w(0, 1)
+            load_w(0, 1)
             nc.sync.dma_start(out=bias_b[:], in_=b_skip.partition_broadcast(P))
-            nc.vector.tensor_copy(out=bias[:], in_=bias_b[:])
+            load_w(1, 0)
+            load_x(1)
 
             wsg = wsraw[:, 4 * C : 8 * C]
             nc.vector.tensor_copy(
@@ -202,88 +306,86 @@ def tile_waveletblock1d_t_kernel(tc, x, w_approx, w_detail, W_skip, b_skip, out)
             )
             nc.vector.quantize_mx(out=ws_codes[:].bitcast(FP8X4), scales=ws_scales[:], in_=wsg)
 
-            tts = {}
             for g in range(4):
-                s, oh = divmod(g, 2)
-                for oq in (2 * oh, 2 * oh + 1):
-                    if (s, oq) not in raws:
-                        raws[(s, oq)] = load_w(s, oq)
+                lay_w(g, 0, 0, "s")
+                if g > 0:
+                    if g < 3:
+                        sum0(g - 1)
+                        keep0(g - 1)
+                lay_w(g, 0, 1, "s")
+                lay_w(g, 1, 0, "s")
+                if g == 0:
+                    load_w(1, 1)
+                    load_w(2, 0)
+                    load_x(2)
+                if g == 1:
+                    load_w(2, 1)
+                    load_w(3, 0)
+                if g == 2:
+                    load_w(3, 1)
+                    load_x(3)
+                    load_x(4)
                 if g < 3:
-                    load_x(g + 1)
-                for lh in range(2):
-                    wg = wstage.tile([P, 4096], BF16, align_bytes=64, tag="wg", name="wg%d_%d" % (g, lh))
-                    for i in range(2):
-                        raw = raws[(s, 2 * oh + i)]
-                        srcv = raw[:].rearrange("p (t o l) -> p o l t", t=4, l=8)[:, :, 4 * lh : 4 * lh + 4]
-                        dstv = wg[:].rearrange("p (l o t) -> p o l t", l=4, t=4)[:, i * P : (i + 1) * P]
-                        if lh == 1 and i == 1:
-                            nc.vector.tensor_copy(out=dstv, in_=srcv)
-                        else:
-                            nc.scalar.copy(out=dstv, in_=srcv)
-                    nc.vector.quantize_mx(
-                        out=w_codes[s][oh][lh][:].bitcast(FP8X4), scales=w_scales[s][oh][lh][:], in_=wg[:]
-                    )
-                if g < 3:
-                    pre_x(g, "vvvv")
-                    haar(g)
-                    tts[(g, 0)] = early(g, 0)
+                    for jp in range(4):
+                        turn_x(g, jp, "v")
+                    quant_x(g)
+                    if g < 2:
+                        sum1(g)
+                lay_w(g, 1, 1, "v")
+                quant_w(g, 0)
+                if g == 1:
+                    early(0, 0)
+                if g == 2:
+                    early(0, 1)
+                if g in (1, 2):
+                    make_a(g - 1)
+                quant_w(g, 1)
+
+            bias = pool1.tile([P, C], F32, tag="pp", name="bias")
+            nc.vector.tensor_copy(out=bias[:], in_=bias_b[:])
+            bp = ps_2.tile([P, C], F32, tag="tin", name="bp")
+            for ob in range(4):
+                nc.tensor.transpose(bp[:, ob * P : (ob + 1) * P], bias[:, ob * P : (ob + 1) * P], ident[:])
+            nc.scalar.mul(bias_t[:], bp[:], -4.0)
 
         zpool = ctx.enter_context(tc.tile_pool(name="zpool", bufs=4))
 
-        def post(u):
-            xu = xus[u]
-            ac, asc, n = state[u][2:5]
-            cc = hpool.tile([P, 2 * C], F32, tag="cc", name="cc%d" % u)
-            lh, li = divmod(u, 4)
-            cols = slice(li * 256, (li + 1) * 256)
-            for h in range(2):
-                mx = ps_1.tile([P, C], F32, tag="mix", name="mix%d_%d" % (u, h))
-                for oh in range(2):
-                    for s in range(2):
-                        a0 = (0, 1 + h)[s] * P
-                        nc.tensor.matmul_mx(
-                            out=mx[:, oh * 256 : (oh + 1) * 256],
-                            lhsT=ac[:, a0 : a0 + P].bitcast(FP8X4),
-                            lhsT_scale=asc[:, a0 : a0 + P],
-                            rhs=w_codes[s][oh][lh][:, cols].bitcast(FP8X4),
-                            rhs_scale=w_scales[s][oh][lh][:, cols],
-                            start=(s == 0),
-                            stop=(s == 1),
-                        )
-                nc.vector.scalar_tensor_tensor(
-                    out=cc[:, h * C : (h + 1) * C],
-                    in0=mx[:],
-                    scalar=R3,
-                    in1=n[:, h * C : (h + 1) * C],
-                    op0=ALU.mult,
-                    op1=ALU.add,
-                )
-            z = zpool.tile([P, 4 * C], F32, tag="z", name="z%d" % u)
-            nc.gpsimd.tensor_tensor(
-                out=z[:].rearrange("p (j c) -> p j c", c=C),
-                in0=xu[:, 4 * C : 8 * C].rearrange("p (j c) -> p j c", c=C),
-                in1=wide(cc[:, C : 2 * C]),
-                op=ALU.add,
-            )
-            tt = tts[(u, 0)] if (u, 0) in tts else early(u, 0)
-            nc.vector.tensor_tensor(
-                out=tt[:].rearrange("p (j c) -> p j c", c=C),
-                in0=tt[:].rearrange("p (j c) -> p j c", c=C),
-                in1=wide(cc[:, 0:C]),
-                op=ALU.add,
-            )
-            finish(u, 0, tt)
-            for jj in range(4):
-                sk = skip(u, 4 + jj)
-                nc.vector.tensor_tensor(
-                    out=z[:, jj * C : (jj + 1) * C], in0=sk[:], in1=z[:, jj * C : (jj + 1) * C], op=ALU.add
-                )
-            finish(u, 1, z)
-
-        for u in range(UNITS):
-            if u + AHEAD < UNITS:
-                if u > 0:
-                    load_x(u + AHEAD)
-                pre_x(u + AHEAD, "ssss")
-                haar(u + AHEAD)
-            post(u)
+        for h in range(2):
+            mix(0, h)
+        for h in range(2):
+            coarse(0, h)
+        for i in range(UNITS):
+            nxt, mid, far = i + 1 < UNITS, i + 2 < UNITS, i + 3 < UNITS
+            if i > 0 and i + 4 < UNITS:
+                load_x(i + 4)
+            if mid:
+                sum1(i + 2)
+            if nxt:
+                mix(i + 1, 0)
+            add_coarse(i, 0)
+            finish(i, 0)
+            if nxt:
+                mix(i + 1, 1)
+            if far:
+                turn_x(i + 3, 0, "s")
+                turn_x(i + 3, 1, "s")
+            if i == 0:
+                add_coarse(i, 1)
+            else:
+                add_skip(i, 1)
+            finish(i, 1)
+            if nxt:
+                coarse(i + 1, 1)
+                pool_add(i + 1, 1)
+                coarse(i + 1, 0)
+            if far:
+                turn_x(i + 3, 2, "s")
+                turn_x(i + 3, 3, "s")
+            if nxt:
+                early(i + 1, 0)
+            if mid:
+                sum0(i + 2)
+                keep0(i + 2)
+                make_a(i + 2)
+            if far:
+                quant_x(i + 3)

@@ -55,10 +55,13 @@ def tile_waveletblock1d_t_kernel(tc, x, w_approx, w_detail, W_skip, b_skip, out)
 
         xus = {}
         xgs = {}
+        tins = {}
+        mixed = {}
         xqs = {}
         s0ps = {}
         s0s = {}
         s1s = {}
+        s1rs = {}
         aqs = {}
         cts = {}
         cps = {}
@@ -69,7 +72,7 @@ def tile_waveletblock1d_t_kernel(tc, x, w_approx, w_detail, W_skip, b_skip, out)
             nc.sync.dma_start(out=xu[:], in_=x[:, 8 * u : 8 * u + 8, :].rearrange("b l c -> b (l c)"))
             xus[u] = xu
 
-        def turn_x(u, jp, engine):
+        def turn_mm(u, jp):
             if jp == 0:
                 xg = pool2.tile([P, 8 * C], BF16, align_bytes=64, tag="xg", name="xg%d" % u)
                 xgs[u] = xg
@@ -83,6 +86,10 @@ def tile_waveletblock1d_t_kernel(tc, x, w_approx, w_detail, W_skip, b_skip, out)
                         xw[:, j * 256 + uu : (j + 1) * 256 : 2],
                         ident[:],
                     )
+            tins[u, jp] = tin
+
+        def turn_copy(u, jp, engine):
+            tin = tins[u, jp]
             dst = xgs[u][:].bitcast(F32)[:, jp * C : (jp + 1) * C].rearrange("p (n u) -> p n u", u=2)
             srcv = tin[:].rearrange("p (u n) -> p n u", u=2)
             if engine == "v":
@@ -90,24 +97,32 @@ def tile_waveletblock1d_t_kernel(tc, x, w_approx, w_detail, W_skip, b_skip, out)
             else:
                 nc.scalar.copy(out=dst, in_=srcv)
 
+        def turn_x(u, jp, engine):
+            turn_mm(u, jp)
+            turn_copy(u, jp, engine)
+
         def quant_x(u):
             xc = pool4.tile([P, 8 * P], U32, align_bytes=64, tag="xc", name="xc%d" % u)
             xs = pool4.tile([P, 8 * P], U8, align_bytes=64, tag="xs", name="xs%d" % u)
             nc.vector.quantize_mx(out=xc[:].bitcast(FP8X4), scales=xs[:], in_=xgs[u][:])
             xqs[u] = (xc, xs)
 
+        def sum0_part(u, t):
+            if t == 0:
+                s0p = ps_1.tile([P, C], F32, tag="s0p", name="s0p%d" % u)
+                s0ps[u] = s0p
+            for j in range(4):
+                nc.tensor.matmul(
+                    s0ps[u][:, t * P : (t + 1) * P],
+                    xus[u][:, j * C + t : (j + 1) * C : 4],
+                    ident_b[:],
+                    start=(j == 0),
+                    stop=(j == 3),
+                )
+
         def sum0(u):
-            s0p = ps_1.tile([P, C], F32, tag="s0p", name="s0p%d" % u)
             for t in range(4):
-                for j in range(4):
-                    nc.tensor.matmul(
-                        s0p[:, t * P : (t + 1) * P],
-                        xus[u][:, j * C + t : (j + 1) * C : 4],
-                        ident_b[:],
-                        start=(j == 0),
-                        stop=(j == 3),
-                    )
-            s0ps[u] = s0p
+                sum0_part(u, t)
 
         def keep0(u):
             s0 = pool2.tile([P, C], F32, tag="s0", name="s0_%d" % u)
@@ -127,10 +142,12 @@ def tile_waveletblock1d_t_kernel(tc, x, w_approx, w_detail, W_skip, b_skip, out)
             s1 = pool2.tile([P, C], F32, tag="s1", name="s1_%d" % u)
             nc.gpsimd.tensor_tensor(out=s1[:], in0=pp[:, 0:C], in1=pp[:, C : 2 * C], op=ALU.add)
             s1s[u] = s1
+            s1r = pool1.tile([P, C], F32, tag="s1r", name="s1r%d" % u)
+            nc.gpsimd.tensor_scalar(out=s1r[:], in0=s1[:], scalar1=R3, scalar2=0.0, op0=ALU.mult, op1=ALU.add)
+            s1rs[u] = s1r
 
         def make_a(u):
-            s1r = pool1.tile([P, C], F32, tag="s1r", name="s1r%d" % u)
-            nc.vector.tensor_scalar(out=s1r[:], in0=s1s[u][:], scalar1=R3, scalar2=None, op0=ALU.mult)
+            s1r = s1rs[u]
             gq = pool2.tile([P, 3 * C], BF16, align_bytes=64, tag="gq", name="gq%d" % u)
             for s in (1, 0):
                 nc.vector.scalar_tensor_tensor(
@@ -169,8 +186,11 @@ def tile_waveletblock1d_t_kernel(tc, x, w_approx, w_detail, W_skip, b_skip, out)
                         start=(s == 0),
                         stop=(s == 1),
                     )
+            mixed[u, h] = mx
+
+        def mix_copy(u, h):
             ct = pool2.tile([P, C], F32, tag="ct", name="ct%d_%d" % (u, h))
-            nc.scalar.mul(ct[:], mx[:], -4.0 * R3)
+            nc.scalar.mul(ct[:], mixed[u, h][:], -4.0 * R3)
             cts[u, h] = ct
 
         def coarse(u, h):
@@ -210,15 +230,19 @@ def tile_waveletblock1d_t_kernel(tc, x, w_approx, w_detail, W_skip, b_skip, out)
             )
             return sk
 
+        def early_part(u, h, jj):
+            if jj == 0:
+                tt = pool3.tile([P, 4 * C], F32, tag="t", name="t%d_%d" % (u, h))
+                zs[u, h] = tt
+            j = 4 * h + jj
+            sk = skip(u, j)
+            nc.vector.tensor_tensor(
+                out=zs[u, h][:, jj * C : (jj + 1) * C], in0=sk[:], in1=xus[u][:, j * C : (j + 1) * C], op=ALU.add
+            )
+
         def early(u, h):
-            tt = pool3.tile([P, 4 * C], F32, tag="t", name="t%d_%d" % (u, h))
             for jj in range(4):
-                j = 4 * h + jj
-                sk = skip(u, j)
-                nc.vector.tensor_tensor(
-                    out=tt[:, jj * C : (jj + 1) * C], in0=sk[:], in1=xus[u][:, j * C : (j + 1) * C], op=ALU.add
-                )
-            zs[u, h] = tt
+                early_part(u, h, jj)
 
         def wide(ap):
             return ap.unsqueeze(1).to_broadcast([P, 4, C])
@@ -233,28 +257,26 @@ def tile_waveletblock1d_t_kernel(tc, x, w_approx, w_detail, W_skip, b_skip, out)
             cc = pool2.tile([P, C], F32, tag="cc", name="cc%d" % u)
             nc.scalar.mul(cc[:], cps[u, h][:], -0.25)
             z = zpool.tile([P, 4 * C], F32, tag="z", name="z%d" % u)
-            nc.gpsimd.tensor_tensor(
-                out=z[:].rearrange("p (j c) -> p j c", c=C),
-                in0=xus[u][:, 4 * h * C : 4 * (h + 1) * C].rearrange("p (j c) -> p j c", c=C),
-                in1=wide(cc[:]),
-                op=ALU.add,
-            )
+            for jj in range(4):
+                j = 4 * h + jj
+                nc.gpsimd.tensor_tensor(
+                    out=z[:, jj * C : (jj + 1) * C], in0=xus[u][:, j * C : (j + 1) * C], in1=cc[:], op=ALU.add
+                )
             zs[u, h] = z
 
-        def add_skip(u, h):
+        def add_skip_part(u, h, jj):
             z = zs[u, h]
-            for jj in range(4):
-                sk = skip(u, 4 * h + jj)
-                nc.vector.tensor_tensor(
-                    out=z[:, jj * C : (jj + 1) * C], in0=sk[:], in1=z[:, jj * C : (jj + 1) * C], op=ALU.add
-                )
+            sk = skip(u, 4 * h + jj)
+            nc.vector.tensor_tensor(
+                out=z[:, jj * C : (jj + 1) * C], in0=sk[:], in1=z[:, jj * C : (jj + 1) * C], op=ALU.add
+            )
 
         def finish(u, h):
             z = zs[u, h]
             nc.scalar.activation(out=z[:], in_=z[:], func=ACT.Gelu_apprx_tanh)
             nc.sync.dma_start(out=out[:, 8 * u + 4 * h : 8 * u + 4 * h + 4, :].rearrange("b l o -> b (l o)"), in_=z[:])
 
-        with tc.tile_pool(name="wstage", bufs=2) as wstage, tc.tile_pool(name="wraw", bufs=3) as rawpool:
+        with tc.tile_pool(name="wstage", bufs=3) as wstage, tc.tile_pool(name="wraw", bufs=4) as rawpool:
             raws = {}
             wgs = {}
 
@@ -287,6 +309,14 @@ def tile_waveletblock1d_t_kernel(tc, x, w_approx, w_detail, W_skip, b_skip, out)
                     out=w_codes[s][oh][lh][:].bitcast(FP8X4), scales=w_scales[s][oh][lh][:], in_=wgs[g, lh][:]
                 )
 
+            def bias_col():
+                bias = pool2.tile([P, C], F32, tag="ct", name="bias")
+                nc.vector.tensor_copy(out=bias[:], in_=bias_b[:])
+                bp = ps_2.tile([P, C], F32, tag="tin", name="bp")
+                for ob in range(4):
+                    nc.tensor.transpose(bp[:, ob * P : (ob + 1) * P], bias[:, ob * P : (ob + 1) * P], ident[:])
+                nc.scalar.mul(bias_t[:], bp[:], -4.0)
+
             load_w(0, 0)
             wsraw = pool2.tile([P, 8 * C], BF16, align_bytes=64, tag="xg", name="wsraw")
             nc.sync.dma_start(
@@ -295,8 +325,9 @@ def tile_waveletblock1d_t_kernel(tc, x, w_approx, w_detail, W_skip, b_skip, out)
             )
             load_x(0)
             load_w(0, 1)
-            nc.sync.dma_start(out=bias_b[:], in_=b_skip.partition_broadcast(P))
             load_w(1, 0)
+            load_w(1, 1)
+            nc.sync.dma_start(out=bias_b[:], in_=b_skip.partition_broadcast(P))
             load_x(1)
 
             wsg = wsraw[:, 4 * C : 8 * C]
@@ -306,86 +337,117 @@ def tile_waveletblock1d_t_kernel(tc, x, w_approx, w_detail, W_skip, b_skip, out)
             )
             nc.vector.quantize_mx(out=ws_codes[:].bitcast(FP8X4), scales=ws_scales[:], in_=wsg)
 
-            for g in range(4):
-                lay_w(g, 0, 0, "s")
-                if g > 0:
-                    if g < 3:
-                        sum0(g - 1)
-                        keep0(g - 1)
-                lay_w(g, 0, 1, "s")
-                lay_w(g, 1, 0, "s")
-                if g == 0:
-                    load_w(1, 1)
-                    load_w(2, 0)
-                    load_x(2)
-                if g == 1:
-                    load_w(2, 1)
-                    load_w(3, 0)
-                if g == 2:
-                    load_w(3, 1)
-                    load_x(3)
-                    load_x(4)
-                if g < 3:
-                    for jp in range(4):
-                        turn_x(g, jp, "v")
-                    quant_x(g)
-                    if g < 2:
-                        sum1(g)
-                lay_w(g, 1, 1, "v")
-                quant_w(g, 0)
-                if g == 1:
-                    early(0, 0)
-                if g == 2:
-                    early(0, 1)
-                if g in (1, 2):
-                    make_a(g - 1)
-                quant_w(g, 1)
-
-            bias = pool1.tile([P, C], F32, tag="pp", name="bias")
-            nc.vector.tensor_copy(out=bias[:], in_=bias_b[:])
-            bp = ps_2.tile([P, C], F32, tag="tin", name="bp")
-            for ob in range(4):
-                nc.tensor.transpose(bp[:, ob * P : (ob + 1) * P], bias[:, ob * P : (ob + 1) * P], ident[:])
-            nc.scalar.mul(bias_t[:], bp[:], -4.0)
+            lay_w(0, 0, 0, "s")
+            lay_w(0, 0, 1, "s")
+            load_w(2, 0)
+            turn_x(0, 0, "v")
+            turn_x(0, 1, "v")
+            turn_x(0, 2, "v")
+            turn_x(0, 3, "v")
+            quant_x(0)
+            sum1(0)
+            sum0(0)
+            lay_w(0, 1, 0, "s")
+            lay_w(0, 1, 1, "v")
+            load_w(2, 1)
+            load_x(2)
+            quant_w(0, 0)
+            quant_w(0, 1)
+            lay_w(1, 0, 0, "s")
+            lay_w(1, 0, 1, "s")
+            load_w(3, 0)
+            keep0(0)
+            bias_col()
+            early(0, 0)
+            lay_w(1, 1, 0, "s")
+            lay_w(1, 1, 1, "v")
+            load_w(3, 1)
+            load_x(3)
+            load_x(4)
+            quant_w(1, 0)
+            quant_w(1, 1)
+            make_a(0)
+            lay_w(2, 0, 0, "s")
+            lay_w(2, 0, 1, "s")
+            turn_x(1, 0, "v")
+            turn_x(1, 1, "v")
+            turn_x(1, 2, "v")
+            turn_x(1, 3, "v")
+            quant_x(1)
+            sum1(1)
+            sum0(1)
+            early(0, 1)
+            lay_w(2, 1, 0, "s")
+            lay_w(2, 1, 1, "v")
+            quant_w(2, 0)
+            quant_w(2, 1)
+            keep0(1)
+            turn_x(2, 0, "v")
+            turn_x(2, 1, "v")
+            turn_x(2, 2, "v")
+            turn_x(2, 3, "v")
+            lay_w(3, 0, 0, "s")
+            lay_w(3, 0, 1, "s")
+            make_a(1)
+            lay_w(3, 1, 0, "s")
+            lay_w(3, 1, 1, "v")
+            quant_w(3, 0)
+            quant_w(3, 1)
+            sum1(2)
 
         zpool = ctx.enter_context(tc.tile_pool(name="zpool", bufs=4))
 
-        for h in range(2):
-            mix(0, h)
-        for h in range(2):
-            coarse(0, h)
+        mix(0, 1)
+        mix_copy(0, 1)
+        early_part(1, 0, 0)
+        early_part(1, 0, 1)
+        mix(0, 0)
+        mix_copy(0, 0)
+        early_part(1, 0, 2)
+        early_part(1, 0, 3)
+        coarse(0, 1)
+        coarse(0, 0)
         for i in range(UNITS):
             nxt, mid, far = i + 1 < UNITS, i + 2 < UNITS, i + 3 < UNITS
             if i > 0 and i + 4 < UNITS:
                 load_x(i + 4)
-            if mid:
+            if mid and i > 0:
                 sum1(i + 2)
-            if nxt:
-                mix(i + 1, 0)
-            add_coarse(i, 0)
-            finish(i, 0)
-            if nxt:
-                mix(i + 1, 1)
-            if far:
-                turn_x(i + 3, 0, "s")
-                turn_x(i + 3, 1, "s")
             if i == 0:
                 add_coarse(i, 1)
             else:
-                add_skip(i, 1)
+                add_skip_part(i, 1, 0)
+                add_skip_part(i, 1, 1)
+            if nxt:
+                mix(i + 1, 1)
+                mix_copy(i + 1, 1)
+            if i > 0:
+                add_skip_part(i, 1, 2)
+                add_skip_part(i, 1, 3)
+            if nxt:
+                mix(i + 1, 0)
             finish(i, 1)
             if nxt:
                 coarse(i + 1, 1)
                 pool_add(i + 1, 1)
-                coarse(i + 1, 0)
+                mix_copy(i + 1, 0)
             if far:
-                turn_x(i + 3, 2, "s")
-                turn_x(i + 3, 3, "s")
-            if nxt:
-                early(i + 1, 0)
+                turn_x(i + 3, 0, "s")
+            add_coarse(i, 0)
+            finish(i, 0)
+            for part in range(4):
+                if nxt and i > 0:
+                    early_part(i + 1, 0, part)
+                if mid and part > 0:
+                    sum0_part(i + 2, part - 1)
             if mid:
-                sum0(i + 2)
+                sum0_part(i + 2, 3)
                 keep0(i + 2)
+            if nxt:
+                coarse(i + 1, 0)
+            for jp in range(1, 4):
+                if far:
+                    turn_x(i + 3, jp, "s")
+            if mid:
                 make_a(i + 2)
-            if far:
-                quant_x(i + 3)
+                quant_x(i + 2)

@@ -40,7 +40,7 @@ def tile_waveletblock1d_t_kernel(tc, x, w_approx, w_detail, W_skip, b_skip, out)
         ident_b = const.tile([P, P], BF16, name="ident_b")
         make_identity(nc, ident_b[:])
         bias_b = const.tile([P, C], BF16, name="bias_b")
-        bias_t = const.tile([P, C], F32, name="bias_t")
+        bias_c = const.tile([P, 4], F32, name="bias_c")
         ws_codes = const.tile([P, C], U32, align_bytes=64, name="ws_codes")
         ws_scales = const.tile([P, C], U8, align_bytes=64, name="ws_scales")
         w_codes = [[[None, None], [None, None]], [[None, None], [None, None]]]
@@ -190,21 +190,28 @@ def tile_waveletblock1d_t_kernel(tc, x, w_approx, w_detail, W_skip, b_skip, out)
 
         def mix_copy(u, h):
             ct = pool2.tile([P, C], F32, tag="ct", name="ct%d_%d" % (u, h))
-            nc.scalar.mul(ct[:], mixed[u, h][:], -4.0 * R3)
+            for ob in range(4):
+                cols = slice(ob * P, (ob + 1) * P)
+                nc.scalar.activation(
+                    out=ct[:, cols],
+                    in_=mixed[u, h][:, cols],
+                    func=ACT.Identity,
+                    scale=-4.0 * R3,
+                    bias=bias_c[:, ob : ob + 1],
+                )
             cts[u, h] = ct
 
         def coarse(u, h):
             cp = ps_2.tile([P, C], F32, tag="cp", name="cp%d_%d" % (u, h))
-            for i, part in enumerate((bias_t, cts[u, h])):
-                for ob in range(4):
-                    nc.tensor.matmul(
-                        cp[:, ob * P : (ob + 1) * P],
-                        part[:, ob * P : (ob + 1) * P],
-                        ident[:],
-                        start=(i == 0 and ob == 0),
-                        stop=False,
-                        is_transpose=True,
-                    )
+            for ob in range(4):
+                nc.tensor.matmul(
+                    cp[:, ob * P : (ob + 1) * P],
+                    cts[u, h][:, ob * P : (ob + 1) * P],
+                    ident[:],
+                    start=(ob == 0),
+                    stop=False,
+                    is_transpose=True,
+                )
             for t in range(4):
                 nc.tensor.matmul(
                     cp[:, t : C : 4],
@@ -315,7 +322,7 @@ def tile_waveletblock1d_t_kernel(tc, x, w_approx, w_detail, W_skip, b_skip, out)
                 bp = ps_2.tile([P, C], F32, tag="tin", name="bp")
                 for ob in range(4):
                     nc.tensor.transpose(bp[:, ob * P : (ob + 1) * P], bias[:, ob * P : (ob + 1) * P], ident[:])
-                nc.scalar.mul(bias_t[:], bp[:], -4.0)
+                nc.scalar.mul(bias_c[:], bp[:, 0:C:P], -4.0)
 
             load_w(0, 0)
             wsraw = pool2.tile([P, 8 * C], BF16, align_bytes=64, tag="xg", name="wsraw")
@@ -381,7 +388,6 @@ def tile_waveletblock1d_t_kernel(tc, x, w_approx, w_detail, W_skip, b_skip, out)
             lay_w(2, 1, 1, "v")
             quant_w(2, 0)
             quant_w(2, 1)
-            keep0(1)
             turn_x(2, 0, "v")
             turn_x(2, 1, "v")
             turn_x(2, 2, "v")
@@ -413,6 +419,8 @@ def tile_waveletblock1d_t_kernel(tc, x, w_approx, w_detail, W_skip, b_skip, out)
                 load_x(i + 4)
             if mid and i > 0:
                 sum1(i + 2)
+            if nxt:
+                keep0(i + 1)
             if i == 0:
                 add_coarse(i, 1)
             else:
@@ -421,6 +429,8 @@ def tile_waveletblock1d_t_kernel(tc, x, w_approx, w_detail, W_skip, b_skip, out)
             if nxt:
                 mix(i + 1, 1)
                 mix_copy(i + 1, 1)
+            if far:
+                turn_x(i + 3, 0, "s")
             if i > 0:
                 add_skip_part(i, 1, 2)
                 add_skip_part(i, 1, 3)
@@ -431,21 +441,19 @@ def tile_waveletblock1d_t_kernel(tc, x, w_approx, w_detail, W_skip, b_skip, out)
                 coarse(i + 1, 1)
                 pool_add(i + 1, 1)
                 mix_copy(i + 1, 0)
-            if far:
-                turn_x(i + 3, 0, "s")
             add_coarse(i, 0)
             finish(i, 0)
             for part in range(4):
                 if nxt and i > 0:
                     early_part(i + 1, 0, part)
-                if mid and part > 0:
-                    sum0_part(i + 2, part - 1)
-            if mid:
-                sum0_part(i + 2, 3)
-                keep0(i + 2)
+                if mid:
+                    sum0_part(i + 2, part)
+                if part == 1:
+                    if far:
+                        turn_x(i + 3, 1, "s")
             if nxt:
                 coarse(i + 1, 0)
-            for jp in range(1, 4):
+            for jp in range(2, 4):
                 if far:
                     turn_x(i + 3, jp, "s")
             if mid:

@@ -16,6 +16,7 @@ C = 512
 UNITS = 8
 R = 0.7071067811865476
 R3 = R * R * R
+POOLED = (1, 2, 3, 4, 5, 6)
 FLOPS = 2 * 8192 * 512 * 512 + 2 * 2 * 8 * 128 * 512 * 512
 
 
@@ -107,37 +108,31 @@ def tile_waveletblock1d_t_kernel(tc, x, w_approx, w_detail, W_skip, b_skip, out)
             nc.vector.quantize_mx(out=xc[:].bitcast(FP8X4), scales=xs[:], in_=xgs[u][:])
             xqs[u] = (xc, xs)
 
-        def sum0_part(u, t):
-            if t == 0:
+        def sum0_part(u, j):
+            if j == 0:
                 s0p = ps_1.tile([P, C], F32, tag="s0p", name="s0p%d" % u)
                 s0ps[u] = s0p
-            for j in range(4):
-                nc.tensor.matmul(
-                    s0ps[u][:, t * P : (t + 1) * P],
-                    xus[u][:, j * C + t : (j + 1) * C : 4],
-                    ident_b[:],
-                    start=(j == 0),
-                    stop=(j == 3),
-                )
+            nc.tensor.matmul(
+                s0ps[u][:], ident_b[:], xgs[u][:, j * C : (j + 1) * C], start=(j == 0), stop=(j == 3)
+            )
 
         def sum0(u):
-            for t in range(4):
-                sum0_part(u, t)
+            for j in range(4):
+                sum0_part(u, j)
 
         def keep0(u):
             s0 = pool2.tile([P, C], F32, tag="s0", name="s0_%d" % u)
-            nc.scalar.copy(out=s0[:], in_=s0ps[u][:])
+            nc.scalar.copy(
+                out=s0[:].rearrange("p (t b) -> p t b", t=4), in_=s0ps[u][:].rearrange("p (b t) -> p t b", t=4)
+            )
             s0s[u] = s0
 
         def sum1(u):
-            xv = xgs[u][:, 4 * C : 8 * C].rearrange("p (k two b t) -> p k two t b", two=2, b=P, t=4)
+            xv = xgs[u][:, 4 * C : 8 * C].rearrange("p (k two c) -> p k two c", two=2, c=C)
             pp = pool1.tile([P, 2 * C], F32, tag="pp", name="pp%d" % u)
             for k in range(2):
                 nc.gpsimd.tensor_tensor(
-                    out=pp[:, k * C : (k + 1) * C].rearrange("p (t b) -> p t b", t=4),
-                    in0=xv[:, k, 0],
-                    in1=xv[:, k, 1],
-                    op=ALU.add,
+                    out=pp[:, k * C : (k + 1) * C], in0=xv[:, k, 0], in1=xv[:, k, 1], op=ALU.add
                 )
             s1 = pool2.tile([P, C], F32, tag="s1", name="s1_%d" % u)
             nc.gpsimd.tensor_tensor(out=s1[:], in0=pp[:, 0:C], in1=pp[:, C : 2 * C], op=ALU.add)
@@ -151,10 +146,10 @@ def tile_waveletblock1d_t_kernel(tc, x, w_approx, w_detail, W_skip, b_skip, out)
             gq = pool2.tile([P, 3 * C], BF16, align_bytes=64, tag="gq", name="gq%d" % u)
             for s in (1, 0):
                 nc.vector.scalar_tensor_tensor(
-                    out=gq[:, s * C : (s + 1) * C].rearrange("p (b t) -> p b t", t=4),
-                    in0=s0ps[u][:].rearrange("p (t b) -> p b t", t=4),
+                    out=gq[:, s * C : (s + 1) * C],
+                    in0=s0ps[u][:],
                     scalar=R3,
-                    in1=s1r[:].rearrange("p (t b) -> p b t", t=4),
+                    in1=s1r[:],
                     op0=ALU.mult,
                     op1=(ALU.add, ALU.subtract)[s],
                 )
@@ -174,7 +169,7 @@ def tile_waveletblock1d_t_kernel(tc, x, w_approx, w_detail, W_skip, b_skip, out)
             lh, li = divmod(u, 4)
             mx = ps_1.tile([P, C], F32, tag="mix", name="mix%d_%d" % (u, h))
             for ob in range(4):
-                w0 = li * 256 + (ob % 2) * P
+                w0 = (ob % 2) * 512 + li * P
                 for s in range(2):
                     a0 = (0, 1 + h)[s] * P
                     nc.tensor.matmul_mx(
@@ -215,7 +210,7 @@ def tile_waveletblock1d_t_kernel(tc, x, w_approx, w_detail, W_skip, b_skip, out)
             for t in range(4):
                 nc.tensor.matmul(
                     cp[:, t : C : 4],
-                    (s0s, s1s)[h][u][:, t * P : (t + 1) * P],
+                    s0s[u][:, t * P : (t + 1) * P] if h == 0 else s1s[u][:, t : C : 4],
                     ident[:],
                     start=False,
                     stop=(t == 3),
@@ -251,13 +246,13 @@ def tile_waveletblock1d_t_kernel(tc, x, w_approx, w_detail, W_skip, b_skip, out)
             for jj in range(4):
                 early_part(u, h, jj)
 
-        def wide(ap):
-            return ap.unsqueeze(1).to_broadcast([P, 4, C])
+        def wide(ap, n):
+            return ap.unsqueeze(1).to_broadcast([P, n, C])
 
-        def add_coarse(u, h):
-            z4 = zs[u, h][:].rearrange("p (j c) -> p j c", c=C)
+        def add_coarse(u, h, j0=0, j1=4):
+            z4 = zs[u, h][:, j0 * C : j1 * C].rearrange("p (j c) -> p j c", c=C)
             nc.vector.scalar_tensor_tensor(
-                out=z4, in0=wide(cps[u, h][:]), scalar=-0.25, in1=z4, op0=ALU.mult, op1=ALU.add
+                out=z4, in0=wide(cps[u, h][:], j1 - j0), scalar=-0.25, in1=z4, op0=ALU.mult, op1=ALU.add
             )
 
         def pool_add(u, h):
@@ -278,10 +273,11 @@ def tile_waveletblock1d_t_kernel(tc, x, w_approx, w_detail, W_skip, b_skip, out)
                 out=z[:, jj * C : (jj + 1) * C], in0=sk[:], in1=z[:, jj * C : (jj + 1) * C], op=ALU.add
             )
 
-        def finish(u, h):
-            z = zs[u, h]
-            nc.scalar.activation(out=z[:], in_=z[:], func=ACT.Gelu_apprx_tanh)
-            nc.sync.dma_start(out=out[:, 8 * u + 4 * h : 8 * u + 4 * h + 4, :].rearrange("b l o -> b (l o)"), in_=z[:])
+        def finish(u, h, j0=0, j1=4):
+            z = zs[u, h][:, j0 * C : j1 * C]
+            nc.scalar.activation(out=z, in_=z, func=ACT.Gelu_apprx_tanh)
+            l0 = 8 * u + 4 * h
+            nc.sync.dma_start(out=out[:, l0 + j0 : l0 + j1, :].rearrange("b l o -> b (l o)"), in_=z)
 
         with tc.tile_pool(name="wstage", bufs=3) as wstage, tc.tile_pool(name="wraw", bufs=4) as rawpool:
             raws = {}
@@ -304,9 +300,11 @@ def tile_waveletblock1d_t_kernel(tc, x, w_approx, w_detail, W_skip, b_skip, out)
                     wg = wstage.tile([P, 4096], BF16, align_bytes=64, tag="wg", name="wg%d_%d" % (g, lh))
                     wgs[g, lh] = wg
                 srcv = raws[g, i][:].rearrange("p (t o l) -> p o l t", t=4, l=8)[:, :, 4 * lh : 4 * lh + 4]
-                dstv = wgs[g, lh][:].rearrange("p (l o t) -> p o l t", l=4, t=4)[:, i * P : (i + 1) * P]
+                dstv = wgs[g, lh][:, i * 2048 : (i + 1) * 2048].rearrange("p (l o t) -> p o l t", l=4, t=4)
                 if engine == "v":
                     nc.vector.tensor_copy(out=dstv, in_=srcv)
+                elif engine == "g":
+                    nc.gpsimd.tensor_scalar(out=dstv, in0=srcv, scalar1=1.0, scalar2=0.0, op0=ALU.mult, op1=ALU.add)
                 else:
                     nc.scalar.copy(out=dstv, in_=srcv)
 
@@ -324,13 +322,13 @@ def tile_waveletblock1d_t_kernel(tc, x, w_approx, w_detail, W_skip, b_skip, out)
                     nc.tensor.transpose(bp[:, ob * P : (ob + 1) * P], bias[:, ob * P : (ob + 1) * P], ident[:])
                 nc.scalar.mul(bias_c[:], bp[:, 0:C:P], -4.0)
 
-            load_w(0, 0)
             wsraw = pool2.tile([P, 8 * C], BF16, align_bytes=64, tag="xg", name="wsraw")
             nc.sync.dma_start(
                 out=wsraw[:, 0 : 4 * C].rearrange("p (t o) -> p t o", t=4),
                 in_=W_skip.rearrange("(q t) o -> q t o", t=4),
             )
             load_x(0)
+            load_w(0, 0)
             load_w(0, 1)
             load_w(1, 0)
             load_w(1, 1)
@@ -344,57 +342,57 @@ def tile_waveletblock1d_t_kernel(tc, x, w_approx, w_detail, W_skip, b_skip, out)
             )
             nc.vector.quantize_mx(out=ws_codes[:].bitcast(FP8X4), scales=ws_scales[:], in_=wsg)
 
+            turn_x(0, 0, "s")
+            turn_x(0, 1, "v")
+            turn_x(0, 2, "s")
+            turn_x(0, 3, "v")
+            quant_x(0)
+            sum0(0)
+            sum1(0)
             lay_w(0, 0, 0, "s")
             lay_w(0, 0, 1, "s")
             load_w(2, 0)
-            turn_x(0, 0, "v")
-            turn_x(0, 1, "v")
-            turn_x(0, 2, "v")
-            turn_x(0, 3, "v")
-            quant_x(0)
-            sum1(0)
-            sum0(0)
+            early(0, 0)
             lay_w(0, 1, 0, "s")
             lay_w(0, 1, 1, "v")
             load_w(2, 1)
             load_x(2)
+            early(0, 1)
             quant_w(0, 0)
             quant_w(0, 1)
             lay_w(1, 0, 0, "s")
-            lay_w(1, 0, 1, "s")
-            load_w(3, 0)
             keep0(0)
             bias_col()
-            early(0, 0)
+            make_a(0)
+            lay_w(1, 0, 1, "s")
+            load_w(3, 0)
             lay_w(1, 1, 0, "s")
             lay_w(1, 1, 1, "v")
             load_w(3, 1)
             load_x(3)
             load_x(4)
-            quant_w(1, 0)
-            quant_w(1, 1)
-            make_a(0)
-            lay_w(2, 0, 0, "s")
-            lay_w(2, 0, 1, "s")
             turn_x(1, 0, "v")
             turn_x(1, 1, "v")
+            quant_w(1, 0)
             turn_x(1, 2, "v")
             turn_x(1, 3, "v")
+            quant_w(1, 1)
             quant_x(1)
             sum1(1)
             sum0(1)
-            early(0, 1)
+            lay_w(2, 0, 0, "s")
+            lay_w(2, 0, 1, "s")
             lay_w(2, 1, 0, "s")
             lay_w(2, 1, 1, "v")
-            quant_w(2, 0)
-            quant_w(2, 1)
             turn_x(2, 0, "v")
             turn_x(2, 1, "v")
+            quant_w(2, 0)
+            quant_w(2, 1)
             turn_x(2, 2, "v")
             turn_x(2, 3, "v")
             lay_w(3, 0, 0, "s")
-            lay_w(3, 0, 1, "s")
             make_a(1)
+            lay_w(3, 0, 1, "s")
             lay_w(3, 1, 0, "s")
             lay_w(3, 1, 1, "v")
             quant_w(3, 0)
@@ -411,9 +409,11 @@ def tile_waveletblock1d_t_kernel(tc, x, w_approx, w_detail, W_skip, b_skip, out)
         mix_copy(0, 0)
         early_part(1, 0, 2)
         early_part(1, 0, 3)
+        quant_x(2)
         coarse(0, 1)
         coarse(0, 0)
         for i in range(UNITS):
+            pooled, next_pooled = i in POOLED, i + 1 in POOLED
             nxt, mid, far = i + 1 < UNITS, i + 2 < UNITS, i + 3 < UNITS
             if i > 0 and i + 4 < UNITS:
                 load_x(i + 4)
@@ -421,28 +421,35 @@ def tile_waveletblock1d_t_kernel(tc, x, w_approx, w_detail, W_skip, b_skip, out)
                 sum1(i + 2)
             if nxt:
                 keep0(i + 1)
-            if i == 0:
-                add_coarse(i, 1)
-            else:
+            if pooled:
                 add_skip_part(i, 1, 0)
                 add_skip_part(i, 1, 1)
+            elif nxt:
+                add_coarse(i, 1)
             if nxt:
                 mix(i + 1, 1)
                 mix_copy(i + 1, 1)
             if far:
                 turn_x(i + 3, 0, "s")
-            if i > 0:
+            if pooled:
                 add_skip_part(i, 1, 2)
                 add_skip_part(i, 1, 3)
             if nxt:
                 mix(i + 1, 0)
-            finish(i, 1)
             if nxt:
+                finish(i, 1)
                 coarse(i + 1, 1)
-                pool_add(i + 1, 1)
+                if next_pooled:
+                    pool_add(i + 1, 1)
                 mix_copy(i + 1, 0)
-            add_coarse(i, 0)
-            finish(i, 0)
+            if nxt:
+                add_coarse(i, 0)
+                finish(i, 0)
+            else:
+                for h in (1, 0):
+                    for j0 in (0, 2):
+                        add_coarse(i, h, j0, j0 + 2)
+                        finish(i, h, j0, j0 + 2)
             for part in range(4):
                 if nxt and i > 0:
                     early_part(i + 1, 0, part)
@@ -451,6 +458,8 @@ def tile_waveletblock1d_t_kernel(tc, x, w_approx, w_detail, W_skip, b_skip, out)
                 if part == 1:
                     if far:
                         turn_x(i + 3, 1, "s")
+            if nxt and i > 0 and not next_pooled:
+                early(i + 1, 1)
             if nxt:
                 coarse(i + 1, 0)
             for jp in range(2, 4):
@@ -458,4 +467,5 @@ def tile_waveletblock1d_t_kernel(tc, x, w_approx, w_detail, W_skip, b_skip, out)
                     turn_x(i + 3, jp, "s")
             if mid:
                 make_a(i + 2)
+            if mid and i > 0:
                 quant_x(i + 2)

@@ -58,6 +58,7 @@ def tile_waveletblock1d_t_kernel(tc, x, w_approx, w_detail, W_skip, b_skip, out)
         xgs = {}
         tins = {}
         mixed = {}
+        ahead = {}
         xqs = {}
         s0ps = {}
         s0s = {}
@@ -266,9 +267,12 @@ def tile_waveletblock1d_t_kernel(tc, x, w_approx, w_detail, W_skip, b_skip, out)
                 )
             zs[u, h] = z
 
+        def skip_ahead(u, h, jj):
+            ahead[u, h, jj] = skip(u, 4 * h + jj)
+
         def add_skip_part(u, h, jj):
             z = zs[u, h]
-            sk = skip(u, 4 * h + jj)
+            sk = ahead[u, h, jj] if (u, h, jj) in ahead else skip(u, 4 * h + jj)
             nc.vector.tensor_tensor(
                 out=z[:, jj * C : (jj + 1) * C], in0=sk[:], in1=z[:, jj * C : (jj + 1) * C], op=ALU.add
             )
@@ -354,20 +358,20 @@ def tile_waveletblock1d_t_kernel(tc, x, w_approx, w_detail, W_skip, b_skip, out)
             load_w(2, 0)
             early(0, 0)
             lay_w(0, 1, 0, "s")
-            lay_w(0, 1, 1, "v")
+            lay_w(0, 1, 1, "g")
             load_w(2, 1)
             load_x(2)
             early(0, 1)
-            quant_w(0, 0)
-            quant_w(0, 1)
             lay_w(1, 0, 0, "s")
-            keep0(0)
             bias_col()
+            keep0(0)
+            quant_w(0, 0)
             make_a(0)
             lay_w(1, 0, 1, "s")
             load_w(3, 0)
+            quant_w(0, 1)
             lay_w(1, 1, 0, "s")
-            lay_w(1, 1, 1, "v")
+            lay_w(1, 1, 1, "g")
             load_w(3, 1)
             load_x(3)
             load_x(4)
@@ -376,22 +380,22 @@ def tile_waveletblock1d_t_kernel(tc, x, w_approx, w_detail, W_skip, b_skip, out)
             quant_w(1, 0)
             turn_x(1, 2, "v")
             turn_x(1, 3, "v")
-            quant_w(1, 1)
             quant_x(1)
-            sum1(1)
             sum0(1)
+            sum1(1)
             lay_w(2, 0, 0, "s")
             lay_w(2, 0, 1, "s")
+            quant_w(1, 1)
             lay_w(2, 1, 0, "s")
             lay_w(2, 1, 1, "v")
             turn_x(2, 0, "v")
             turn_x(2, 1, "v")
             quant_w(2, 0)
-            quant_w(2, 1)
             turn_x(2, 2, "v")
             turn_x(2, 3, "v")
             lay_w(3, 0, 0, "s")
             make_a(1)
+            quant_w(2, 1)
             lay_w(3, 0, 1, "s")
             lay_w(3, 1, 0, "s")
             lay_w(3, 1, 1, "v")
@@ -442,6 +446,8 @@ def tile_waveletblock1d_t_kernel(tc, x, w_approx, w_detail, W_skip, b_skip, out)
                 if next_pooled:
                     pool_add(i + 1, 1)
                 mix_copy(i + 1, 0)
+            if far:
+                turn_x(i + 3, 1, "s")
             if nxt:
                 add_coarse(i, 0)
                 finish(i, 0)
@@ -455,16 +461,17 @@ def tile_waveletblock1d_t_kernel(tc, x, w_approx, w_detail, W_skip, b_skip, out)
                     early_part(i + 1, 0, part)
                 if mid:
                     sum0_part(i + 2, part)
-                if part == 1:
-                    if far:
-                        turn_x(i + 3, 1, "s")
             if nxt and i > 0 and not next_pooled:
                 early(i + 1, 1)
             if nxt:
                 coarse(i + 1, 0)
-            for jp in range(2, 4):
-                if far:
-                    turn_x(i + 3, jp, "s")
+            if far:
+                turn_x(i + 3, 2, "s")
+            if next_pooled:
+                skip_ahead(i + 1, 1, 0)
+                skip_ahead(i + 1, 1, 1)
+            if far:
+                turn_x(i + 3, 3, "s")
             if mid:
                 make_a(i + 2)
             if mid and i > 0:

@@ -17,6 +17,7 @@ UNITS = 8
 R = 0.7071067811865476
 R3 = R * R * R
 POOLED = (1, 2, 3, 4, 5, 6)
+SHARE = 3
 FLOPS = 2 * 8192 * 512 * 512 + 2 * 2 * 8 * 128 * 512 * 512
 
 
@@ -233,10 +234,16 @@ def tile_waveletblock1d_t_kernel(tc, x, w_approx, w_detail, W_skip, b_skip, out)
             )
             return sk
 
+        def open_z(u, h):
+            if h == 1 and u in POOLED:
+                z = zpool.tile([P, 4 * C], F32, tag="z", name="z%d" % u)
+            else:
+                z = pool3.tile([P, 4 * C], F32, tag="t", name="t%d_%d" % (u, h))
+            zs[u, h] = z
+
         def early_part(u, h, jj):
-            if jj == 0:
-                tt = pool3.tile([P, 4 * C], F32, tag="t", name="t%d_%d" % (u, h))
-                zs[u, h] = tt
+            if (u, h) not in zs:
+                open_z(u, h)
             j = 4 * h + jj
             sk = skip(u, j)
             nc.vector.tensor_tensor(
@@ -259,8 +266,8 @@ def tile_waveletblock1d_t_kernel(tc, x, w_approx, w_detail, W_skip, b_skip, out)
         def pool_add(u, h):
             cc = pool2.tile([P, C], F32, tag="cc", name="cc%d" % u)
             nc.scalar.mul(cc[:], cps[u, h][:], -0.25)
-            z = zpool.tile([P, 4 * C], F32, tag="z", name="z%d" % u)
-            for jj in range(4):
+            z = zs[u, h]
+            for jj in range(SHARE):
                 j = 4 * h + jj
                 nc.gpsimd.tensor_tensor(
                     out=z[:, jj * C : (jj + 1) * C], in0=xus[u][:, j * C : (j + 1) * C], in1=cc[:], op=ALU.add
@@ -405,6 +412,8 @@ def tile_waveletblock1d_t_kernel(tc, x, w_approx, w_detail, W_skip, b_skip, out)
 
         zpool = ctx.enter_context(tc.tile_pool(name="zpool", bufs=4))
 
+        turn_x(3, 0, "s")
+        turn_x(3, 1, "s")
         mix(0, 1)
         mix_copy(0, 1)
         early_part(1, 0, 0)
@@ -426,6 +435,7 @@ def tile_waveletblock1d_t_kernel(tc, x, w_approx, w_detail, W_skip, b_skip, out)
             if nxt:
                 keep0(i + 1)
             if pooled:
+                add_coarse(i, 1, SHARE, 4)
                 add_skip_part(i, 1, 0)
                 add_skip_part(i, 1, 1)
             elif nxt:
@@ -433,20 +443,20 @@ def tile_waveletblock1d_t_kernel(tc, x, w_approx, w_detail, W_skip, b_skip, out)
             if nxt:
                 mix(i + 1, 1)
                 mix_copy(i + 1, 1)
-            if far:
+            if far and i > 0:
                 turn_x(i + 3, 0, "s")
-            if pooled:
+            if pooled and SHARE > 2:
                 add_skip_part(i, 1, 2)
-                add_skip_part(i, 1, 3)
             if nxt:
                 mix(i + 1, 0)
             if nxt:
                 finish(i, 1)
                 coarse(i + 1, 1)
                 if next_pooled:
+                    open_z(i + 1, 1)
                     pool_add(i + 1, 1)
                 mix_copy(i + 1, 0)
-            if far:
+            if far and i > 0:
                 turn_x(i + 3, 1, "s")
             if nxt:
                 add_coarse(i, 0)
@@ -461,7 +471,10 @@ def tile_waveletblock1d_t_kernel(tc, x, w_approx, w_detail, W_skip, b_skip, out)
                     early_part(i + 1, 0, part)
                 if mid:
                     sum0_part(i + 2, part)
-            if nxt and i > 0 and not next_pooled:
+            if next_pooled:
+                for jj in range(SHARE, 4):
+                    early_part(i + 1, 1, jj)
+            elif nxt and i > 0:
                 early(i + 1, 1)
             if nxt:
                 coarse(i + 1, 0)

@@ -29,7 +29,7 @@ def tile_waveletblock1d_t_kernel(tc, x, w_approx, w_detail, W_skip, b_skip, out)
         pool1 = ctx.enter_context(tc.tile_pool(name="pool1", bufs=1))
         pool2 = ctx.enter_context(tc.tile_pool(name="pool2", bufs=2))
         pool3 = ctx.enter_context(tc.tile_pool(name="pool3", bufs=3))
-        pool4 = ctx.enter_context(tc.tile_pool(name="pool4", bufs=4))
+        pool4 = ctx.enter_context(tc.tile_pool(name="pool4", bufs=3))
         xpool = ctx.enter_context(tc.tile_pool(name="xpool", bufs=5))
         ps_2 = ctx.enter_context(tc.psum_pool(name="ps_2", bufs=2))
         ps_1 = ctx.enter_context(tc.psum_pool(name="ps_1", bufs=1))
@@ -70,10 +70,13 @@ def tile_waveletblock1d_t_kernel(tc, x, w_approx, w_detail, W_skip, b_skip, out)
         cps = {}
         zs = {}
 
-        def load_x(u):
-            xu = xpool.tile([P, 8 * C], BF16, tag="xu", name="xu%d" % u)
-            nc.sync.dma_start(out=xu[:], in_=x[:, 8 * u : 8 * u + 8, :].rearrange("b l c -> b (l c)"))
-            xus[u] = xu
+        def load_x(u, j0=0, j1=8):
+            if j0 == 0:
+                xu = xpool.tile([P, 8 * C], BF16, tag="xu", name="xu%d" % u)
+                xus[u] = xu
+            nc.sync.dma_start(
+                out=xus[u][:, j0 * C : j1 * C], in_=x[:, 8 * u + j0 : 8 * u + j1, :].rearrange("b l c -> b (l c)")
+            )
 
         def turn_mm(u, jp):
             if jp == 0:
@@ -290,7 +293,7 @@ def tile_waveletblock1d_t_kernel(tc, x, w_approx, w_detail, W_skip, b_skip, out)
             l0 = 8 * u + 4 * h
             nc.sync.dma_start(out=out[:, l0 + j0 : l0 + j1, :].rearrange("b l o -> b (l o)"), in_=z)
 
-        with tc.tile_pool(name="wstage", bufs=3) as wstage, tc.tile_pool(name="wraw", bufs=4) as rawpool:
+        with tc.tile_pool(name="wstage", bufs=4) as wstage, tc.tile_pool(name="wraw", bufs=4) as rawpool:
             raws = {}
             wgs = {}
 
@@ -317,7 +320,7 @@ def tile_waveletblock1d_t_kernel(tc, x, w_approx, w_detail, W_skip, b_skip, out)
                 elif engine == "g":
                     nc.gpsimd.tensor_scalar(out=dstv, in0=srcv, scalar1=1.0, scalar2=0.0, op0=ALU.mult, op1=ALU.add)
                 else:
-                    nc.scalar.copy(out=dstv, in_=srcv)
+                    nc.scalar.copy(out=dstv.rearrange("p o l t -> p o t l"), in_=srcv.rearrange("p o l t -> p o t l"))
 
             def quant_w(g, lh):
                 s, oh = divmod(g, 2)
@@ -333,29 +336,32 @@ def tile_waveletblock1d_t_kernel(tc, x, w_approx, w_detail, W_skip, b_skip, out)
                     nc.tensor.transpose(bp[:, ob * P : (ob + 1) * P], bias[:, ob * P : (ob + 1) * P], ident[:])
                 nc.scalar.mul(bias_c[:], bp[:, 0:C:P], -4.0)
 
+            def quant_skip():
+                wsg = wsraw[:, 4 * C : 8 * C]
+                nc.vector.tensor_copy(
+                    out=wsg.rearrange("p (o t) -> p o t", t=4),
+                    in_=wsraw[:, 0 : 4 * C].rearrange("p (t o) -> p o t", t=4),
+                )
+                nc.vector.quantize_mx(out=ws_codes[:].bitcast(FP8X4), scales=ws_scales[:], in_=wsg)
+
+            load_x(0, 0, 4)
             wsraw = pool2.tile([P, 8 * C], BF16, align_bytes=64, tag="xg", name="wsraw")
             nc.sync.dma_start(
                 out=wsraw[:, 0 : 4 * C].rearrange("p (t o) -> p t o", t=4),
                 in_=W_skip.rearrange("(q t) o -> q t o", t=4),
             )
-            load_x(0)
+            load_x(0, 4, 8)
             load_w(0, 0)
+            nc.sync.dma_start(out=bias_b[:], in_=b_skip.partition_broadcast(P))
             load_w(0, 1)
             load_w(1, 0)
             load_w(1, 1)
-            nc.sync.dma_start(out=bias_b[:], in_=b_skip.partition_broadcast(P))
             load_x(1)
 
-            wsg = wsraw[:, 4 * C : 8 * C]
-            nc.vector.tensor_copy(
-                out=wsg.rearrange("p (o t) -> p o t", t=4),
-                in_=wsraw[:, 0 : 4 * C].rearrange("p (t o) -> p o t", t=4),
-            )
-            nc.vector.quantize_mx(out=ws_codes[:].bitcast(FP8X4), scales=ws_scales[:], in_=wsg)
-
             turn_x(0, 0, "s")
-            turn_x(0, 1, "v")
-            turn_x(0, 2, "s")
+            turn_x(0, 1, "s")
+            quant_skip()
+            turn_x(0, 2, "v")
             turn_x(0, 3, "v")
             quant_x(0)
             sum0(0)
@@ -364,21 +370,21 @@ def tile_waveletblock1d_t_kernel(tc, x, w_approx, w_detail, W_skip, b_skip, out)
             lay_w(0, 0, 1, "s")
             load_w(2, 0)
             early(0, 0)
+            bias_col()
             lay_w(0, 1, 0, "s")
-            lay_w(0, 1, 1, "g")
+            lay_w(0, 1, 1, "v")
             load_w(2, 1)
             load_x(2)
             early(0, 1)
             lay_w(1, 0, 0, "s")
-            bias_col()
-            keep0(0)
             quant_w(0, 0)
             make_a(0)
             lay_w(1, 0, 1, "s")
             load_w(3, 0)
             quant_w(0, 1)
-            lay_w(1, 1, 0, "s")
-            lay_w(1, 1, 1, "g")
+            keep0(0)
+            lay_w(1, 1, 0, "v")
+            lay_w(1, 1, 1, "v")
             load_w(3, 1)
             load_x(3)
             load_x(4)
@@ -387,12 +393,12 @@ def tile_waveletblock1d_t_kernel(tc, x, w_approx, w_detail, W_skip, b_skip, out)
             quant_w(1, 0)
             turn_x(1, 2, "v")
             turn_x(1, 3, "v")
+            quant_w(1, 1)
             quant_x(1)
             sum0(1)
             sum1(1)
             lay_w(2, 0, 0, "s")
             lay_w(2, 0, 1, "s")
-            quant_w(1, 1)
             lay_w(2, 1, 0, "s")
             lay_w(2, 1, 1, "v")
             turn_x(2, 0, "v")

@@ -16,7 +16,6 @@ C = 512
 UNITS = 8
 R = 0.7071067811865476
 R3 = R * R * R
-POOLED = (1, 2, 3, 4, 5, 6)
 SHARE = 3
 FLOPS = 2 * 8192 * 512 * 512 + 2 * 2 * 8 * 128 * 512 * 512
 
@@ -238,7 +237,7 @@ def tile_waveletblock1d_t_kernel(tc, x, w_approx, w_detail, W_skip, b_skip, out)
             return sk
 
         def open_z(u, h):
-            if h == 1 and u in POOLED:
+            if h == 1 and u > 0:
                 z = zpool.tile([P, 4 * C], F32, tag="z", name="z%d" % u)
             else:
                 z = pool3.tile([P, 4 * C], F32, tag="t", name="t%d_%d" % (u, h))
@@ -383,7 +382,7 @@ def tile_waveletblock1d_t_kernel(tc, x, w_approx, w_detail, W_skip, b_skip, out)
             load_w(3, 0)
             quant_w(0, 1)
             keep0(0)
-            lay_w(1, 1, 0, "v")
+            lay_w(1, 1, 0, "g")
             lay_w(1, 1, 1, "v")
             load_w(3, 1)
             load_x(3)
@@ -432,7 +431,6 @@ def tile_waveletblock1d_t_kernel(tc, x, w_approx, w_detail, W_skip, b_skip, out)
         coarse(0, 1)
         coarse(0, 0)
         for i in range(UNITS):
-            pooled, next_pooled = i in POOLED, i + 1 in POOLED
             nxt, mid, far = i + 1 < UNITS, i + 2 < UNITS, i + 3 < UNITS
             if i > 0 and i + 4 < UNITS:
                 load_x(i + 4)
@@ -440,53 +438,50 @@ def tile_waveletblock1d_t_kernel(tc, x, w_approx, w_detail, W_skip, b_skip, out)
                 sum1(i + 2)
             if nxt:
                 keep0(i + 1)
-            if pooled:
+            if i > 0:
                 add_coarse(i, 1, SHARE, 4)
                 add_skip_part(i, 1, 0)
                 add_skip_part(i, 1, 1)
-            elif nxt:
+            else:
                 add_coarse(i, 1)
             if nxt:
                 mix(i + 1, 1)
                 mix_copy(i + 1, 1)
+            else:
+                finish(i, 1, 0, 2)
             if far and i > 0:
                 turn_x(i + 3, 0, "s")
-            if pooled and SHARE > 2:
+            if i > 0:
                 add_skip_part(i, 1, 2)
             if nxt:
                 mix(i + 1, 0)
-            if nxt:
                 finish(i, 1)
                 coarse(i + 1, 1)
-                if next_pooled:
-                    open_z(i + 1, 1)
-                    pool_add(i + 1, 1)
+                open_z(i + 1, 1)
+                pool_add(i + 1, 1)
                 mix_copy(i + 1, 0)
+            else:
+                finish(i, 1, 2, 4)
             if far and i > 0:
                 turn_x(i + 3, 1, "s")
             if nxt:
                 add_coarse(i, 0)
                 finish(i, 0)
             else:
-                for h in (1, 0):
-                    for j0 in (0, 2):
-                        add_coarse(i, h, j0, j0 + 2)
-                        finish(i, h, j0, j0 + 2)
+                for j0 in (0, 2):
+                    add_coarse(i, 0, j0, j0 + 2)
+                    finish(i, 0, j0, j0 + 2)
             for part in range(4):
                 if nxt and i > 0:
                     early_part(i + 1, 0, part)
                 if mid:
                     sum0_part(i + 2, part)
-            if next_pooled:
-                for jj in range(SHARE, 4):
-                    early_part(i + 1, 1, jj)
-            elif nxt and i > 0:
-                early(i + 1, 1)
             if nxt:
+                early_part(i + 1, 1, SHARE)
                 coarse(i + 1, 0)
             if far:
                 turn_x(i + 3, 2, "s")
-            if next_pooled:
+            if nxt:
                 skip_ahead(i + 1, 1, 0)
                 skip_ahead(i + 1, 1, 1)
             if far:

@@ -29,7 +29,7 @@ def tile_waveletblock1d_t_kernel(tc, x, w_approx, w_detail, W_skip, b_skip, out)
         pool2 = ctx.enter_context(tc.tile_pool(name="pool2", bufs=2))
         pool3 = ctx.enter_context(tc.tile_pool(name="pool3", bufs=3))
         pool4 = ctx.enter_context(tc.tile_pool(name="pool4", bufs=3))
-        xpool = ctx.enter_context(tc.tile_pool(name="xpool", bufs=5))
+        xpool = ctx.enter_context(tc.tile_pool(name="xpool", bufs=4))
         ps_2 = ctx.enter_context(tc.psum_pool(name="ps_2", bufs=2))
         ps_1 = ctx.enter_context(tc.psum_pool(name="ps_1", bufs=1))
 
@@ -292,7 +292,7 @@ def tile_waveletblock1d_t_kernel(tc, x, w_approx, w_detail, W_skip, b_skip, out)
             l0 = 8 * u + 4 * h
             nc.sync.dma_start(out=out[:, l0 + j0 : l0 + j1, :].rearrange("b l o -> b (l o)"), in_=z)
 
-        with tc.tile_pool(name="wstage", bufs=4) as wstage, tc.tile_pool(name="wraw", bufs=4) as rawpool:
+        with tc.tile_pool(name="wstage", bufs=5) as wstage, tc.tile_pool(name="wraw", bufs=4) as rawpool:
             raws = {}
             wgs = {}
 
@@ -312,14 +312,21 @@ def tile_waveletblock1d_t_kernel(tc, x, w_approx, w_detail, W_skip, b_skip, out)
                 if i == 0:
                     wg = wstage.tile([P, 4096], BF16, align_bytes=64, tag="wg", name="wg%d_%d" % (g, lh))
                     wgs[g, lh] = wg
-                srcv = raws[g, i][:].rearrange("p (t o l) -> p o l t", t=4, l=8)[:, :, 4 * lh : 4 * lh + 4]
-                dstv = wgs[g, lh][:, i * 2048 : (i + 1) * 2048].rearrange("p (l o t) -> p o l t", l=4, t=4)
+                srcv = raws[g, i][:].rearrange("p (t o l) -> p o t l", t=4, l=8)[:, :, :, 4 * lh : 4 * lh + 4]
+                dstv = wgs[g, lh][:, i * 2048 : (i + 1) * 2048].rearrange("p (l o t) -> p o t l", l=4, t=4)
                 if engine == "v":
                     nc.vector.tensor_copy(out=dstv, in_=srcv)
                 elif engine == "g":
-                    nc.gpsimd.tensor_scalar(out=dstv, in0=srcv, scalar1=1.0, scalar2=0.0, op0=ALU.mult, op1=ALU.add)
+                    nc.gpsimd.tensor_scalar(
+                        out=dstv.rearrange("p o t l -> p o l t"),
+                        in0=srcv.rearrange("p o t l -> p o l t"),
+                        scalar1=1.0,
+                        scalar2=0.0,
+                        op0=ALU.mult,
+                        op1=ALU.add,
+                    )
                 else:
-                    nc.scalar.copy(out=dstv.rearrange("p o l t -> p o t l"), in_=srcv.rearrange("p o l t -> p o t l"))
+                    nc.scalar.copy(out=dstv, in_=srcv)
 
             def quant_w(g, lh):
                 s, oh = divmod(g, 2)
@@ -386,8 +393,7 @@ def tile_waveletblock1d_t_kernel(tc, x, w_approx, w_detail, W_skip, b_skip, out)
             lay_w(1, 1, 1, "v")
             load_w(3, 1)
             load_x(3)
-            load_x(4)
-            turn_x(1, 0, "v")
+            turn_x(1, 0, "s")
             turn_x(1, 1, "v")
             quant_w(1, 0)
             turn_x(1, 2, "v")
@@ -406,33 +412,33 @@ def tile_waveletblock1d_t_kernel(tc, x, w_approx, w_detail, W_skip, b_skip, out)
             turn_x(2, 2, "v")
             turn_x(2, 3, "v")
             lay_w(3, 0, 0, "s")
-            make_a(1)
-            quant_w(2, 1)
-            lay_w(3, 0, 1, "s")
             lay_w(3, 1, 0, "s")
-            lay_w(3, 1, 1, "v")
+            make_a(1)
             quant_w(3, 0)
-            quant_w(3, 1)
+            quant_w(2, 1)
             sum1(2)
+            turn_x(3, 0, "s")
+            turn_x(3, 1, "s")
+            mix(0, 1)
+            mix_copy(0, 1)
+            early_part(1, 0, 0)
+            early_part(1, 0, 1)
+            mix(0, 0)
+            mix_copy(0, 0)
+            early_part(1, 0, 2)
+            early_part(1, 0, 3)
+            lay_w(3, 0, 1, "s")
+            lay_w(3, 1, 1, "v")
+            quant_x(2)
+            quant_w(3, 1)
+            coarse(0, 1)
+            coarse(0, 0)
 
         zpool = ctx.enter_context(tc.tile_pool(name="zpool", bufs=4))
 
-        turn_x(3, 0, "s")
-        turn_x(3, 1, "s")
-        mix(0, 1)
-        mix_copy(0, 1)
-        early_part(1, 0, 0)
-        early_part(1, 0, 1)
-        mix(0, 0)
-        mix_copy(0, 0)
-        early_part(1, 0, 2)
-        early_part(1, 0, 3)
-        quant_x(2)
-        coarse(0, 1)
-        coarse(0, 0)
         for i in range(UNITS):
             nxt, mid, far = i + 1 < UNITS, i + 2 < UNITS, i + 3 < UNITS
-            if i > 0 and i + 4 < UNITS:
+            if i + 4 < UNITS:
                 load_x(i + 4)
             if mid and i > 0:
                 sum1(i + 2)
@@ -471,13 +477,14 @@ def tile_waveletblock1d_t_kernel(tc, x, w_approx, w_detail, W_skip, b_skip, out)
                 for j0 in (0, 2):
                     add_coarse(i, 0, j0, j0 + 2)
                     finish(i, 0, j0, j0 + 2)
+            if nxt:
+                early_part(i + 1, 1, SHARE)
             for part in range(4):
                 if nxt and i > 0:
                     early_part(i + 1, 0, part)
                 if mid:
                     sum0_part(i + 2, part)
             if nxt:
-                early_part(i + 1, 1, SHARE)
                 coarse(i + 1, 0)
             if far:
                 turn_x(i + 3, 2, "s")

@@ -31,7 +31,7 @@ def tile_waveletblock1d_t_kernel(tc, x, w_approx, w_detail, W_skip, b_skip, out)
         pool4 = ctx.enter_context(tc.tile_pool(name="pool4", bufs=3))
         xpool = ctx.enter_context(tc.tile_pool(name="xpool", bufs=4))
         ps_2 = ctx.enter_context(tc.psum_pool(name="ps_2", bufs=2))
-        ps_1 = ctx.enter_context(tc.psum_pool(name="ps_1", bufs=1))
+        ps_4 = ctx.enter_context(tc.psum_pool(name="ps_4", bufs=4))
 
         warm = const.tile([P, 1], F32, name="warm")
         nc.vector.memset(warm[:], 0.0)
@@ -67,6 +67,8 @@ def tile_waveletblock1d_t_kernel(tc, x, w_approx, w_detail, W_skip, b_skip, out)
         aqs = {}
         cts = {}
         cps = {}
+        gqs = {}
+        ccs = {}
         zs = {}
 
         def load_x(u, j0=0, j1=8):
@@ -82,7 +84,7 @@ def tile_waveletblock1d_t_kernel(tc, x, w_approx, w_detail, W_skip, b_skip, out)
                 xg = pool2.tile([P, 8 * C], BF16, align_bytes=64, tag="xg", name="xg%d" % u)
                 xgs[u] = xg
             xw = xus[u][:].bitcast(F32)
-            tin = ps_2.tile([P, C], F32, tag="tin", name="tin%d_%d" % (u, jp))
+            tin = ps_4.tile([P, C], F32, tag="io", name="tin%d_%d" % (u, jp))
             for jj in range(2):
                 j = 2 * jp + jj
                 for uu in range(2):
@@ -114,7 +116,7 @@ def tile_waveletblock1d_t_kernel(tc, x, w_approx, w_detail, W_skip, b_skip, out)
 
         def sum0_part(u, j):
             if j == 0:
-                s0p = ps_1.tile([P, C], F32, tag="s0p", name="s0p%d" % u)
+                s0p = ps_2.tile([P, C], F32, tag="ms", name="s0p%d" % u)
                 s0ps[u] = s0p
             nc.tensor.matmul(
                 s0ps[u][:], ident_b[:], xgs[u][:, j * C : (j + 1) * C], start=(j == 0), stop=(j == 3)
@@ -160,6 +162,10 @@ def tile_waveletblock1d_t_kernel(tc, x, w_approx, w_detail, W_skip, b_skip, out)
             nc.vector.tensor_scalar(
                 out=gq[:, 2 * C : 3 * C], in0=gq[:, C : 2 * C], scalar1=-1.0, scalar2=None, op0=ALU.mult
             )
+            gqs[u] = gq
+
+        def quant_a(u):
+            gq = gqs[u]
             ac = pool2.tile([P, 3 * P], U32, align_bytes=64, tag="ac", name="ac%d" % u)
             asc = pool2.tile([P, 3 * P], U8, align_bytes=64, tag="as", name="as%d" % u)
             nc.vector.quantize_mx(out=ac[:, 0 : 2 * P].bitcast(FP8X4), scales=asc[:, 0 : 2 * P], in_=gq[:, 0 : 2 * C])
@@ -171,7 +177,7 @@ def tile_waveletblock1d_t_kernel(tc, x, w_approx, w_detail, W_skip, b_skip, out)
         def mix(u, h):
             ac, asc = aqs[u]
             lh, li = divmod(u, 4)
-            mx = ps_1.tile([P, C], F32, tag="mix", name="mix%d_%d" % (u, h))
+            mx = ps_2.tile([P, C], F32, tag="ms", name="mix%d_%d" % (u, h))
             for ob in range(4):
                 w0 = (ob % 2) * 512 + li * P
                 for s in range(2):
@@ -223,7 +229,7 @@ def tile_waveletblock1d_t_kernel(tc, x, w_approx, w_detail, W_skip, b_skip, out)
             cps[u, h] = cp
 
         def skip(u, j):
-            sk = ps_2.tile([P, C], F32, tag="sk", name="sk%d_%d" % (u, j))
+            sk = ps_4.tile([P, C], F32, tag="io", name="sk%d_%d" % (u, j))
             xc, xs = xqs[u]
             nc.tensor.matmul_mx(
                 out=sk[:],
@@ -258,6 +264,33 @@ def tile_waveletblock1d_t_kernel(tc, x, w_approx, w_detail, W_skip, b_skip, out)
 
         def wide(ap, n):
             return ap.unsqueeze(1).to_broadcast([P, n, C])
+
+        def sk_t(u, h, jj):
+            ahead[u, h, jj] = skip(u, 4 * h + jj)
+
+        def sk_v(u, h, jj):
+            if (u, h) not in zs:
+                open_z(u, h)
+            j = 4 * h + jj
+            cols = slice(jj * C, (jj + 1) * C)
+            if h == 1 and u > 0 and jj < SHARE:
+                other = zs[u, h][:, cols]
+            else:
+                other = xus[u][:, j * C : (j + 1) * C]
+            nc.vector.tensor_tensor(out=zs[u, h][:, cols], in0=ahead[u, h, jj][:], in1=other, op=ALU.add)
+
+        def copy_coarse(u, h):
+            cc = pool2.tile([P, C], F32, tag="cc", name="cc%d" % u)
+            nc.scalar.mul(cc[:], cps[u, h][:], -0.25)
+            ccs[u, h] = cc
+
+        def g_add(u, h):
+            z = zs[u, h]
+            for jj in range(SHARE):
+                j = 4 * h + jj
+                nc.gpsimd.tensor_tensor(
+                    out=z[:, jj * C : (jj + 1) * C], in0=xus[u][:, j * C : (j + 1) * C], in1=ccs[u, h][:], op=ALU.add
+                )
 
         def add_coarse(u, h, j0=0, j1=4):
             z4 = zs[u, h][:, j0 * C : j1 * C].rearrange("p (j c) -> p j c", c=C)
@@ -337,7 +370,7 @@ def tile_waveletblock1d_t_kernel(tc, x, w_approx, w_detail, W_skip, b_skip, out)
             def bias_col():
                 bias = pool2.tile([P, C], F32, tag="ct", name="bias")
                 nc.vector.tensor_copy(out=bias[:], in_=bias_b[:])
-                bp = ps_2.tile([P, C], F32, tag="tin", name="bp")
+                bp = ps_4.tile([P, C], F32, tag="io", name="bp")
                 for ob in range(4):
                     nc.tensor.transpose(bp[:, ob * P : (ob + 1) * P], bias[:, ob * P : (ob + 1) * P], ident[:])
                 nc.scalar.mul(bias_c[:], bp[:, 0:C:P], -4.0)
@@ -385,6 +418,7 @@ def tile_waveletblock1d_t_kernel(tc, x, w_approx, w_detail, W_skip, b_skip, out)
             lay_w(1, 0, 0, "s")
             quant_w(0, 0)
             make_a(0)
+            quant_a(0)
             lay_w(1, 0, 1, "s")
             load_w(3, 0)
             quant_w(0, 1)
@@ -414,6 +448,8 @@ def tile_waveletblock1d_t_kernel(tc, x, w_approx, w_detail, W_skip, b_skip, out)
             lay_w(3, 0, 0, "s")
             lay_w(3, 1, 0, "s")
             make_a(1)
+            quant_a(1)
+            keep0(1)
             quant_w(3, 0)
             quant_w(2, 1)
             sum1(2)
@@ -438,62 +474,103 @@ def tile_waveletblock1d_t_kernel(tc, x, w_approx, w_detail, W_skip, b_skip, out)
 
         for i in range(UNITS):
             nxt, mid, far = i + 1 < UNITS, i + 2 < UNITS, i + 3 < UNITS
-            if i + 4 < UNITS:
+            if i + 4 < 8:
                 load_x(i + 4)
-            if mid and i > 0:
+            if 0 < i and i + 2 < 8:
                 sum1(i + 2)
-            if nxt:
-                keep0(i + 1)
             if i > 0:
-                add_coarse(i, 1, SHARE, 4)
-                add_skip_part(i, 1, 0)
-                add_skip_part(i, 1, 1)
-            else:
-                add_coarse(i, 1)
-            if nxt:
+                sk_t(i, 1, 2)
+            if i + 1 < 8:
                 mix(i + 1, 1)
-                mix_copy(i + 1, 1)
-            else:
-                finish(i, 1, 0, 2)
-            if far and i > 0:
-                turn_x(i + 3, 0, "s")
+            if i + 1 < 8 and i > 0:
+                keep0(i + 1)
+            if True:
+                add_coarse(i, 1, SHARE if i > 0 else 0, 4)
             if i > 0:
-                add_skip_part(i, 1, 2)
-            if nxt:
+                sk_v(i, 1, 0)
+            if i > 0:
+                sk_v(i, 1, 1)
+            if i > 0:
+                sk_v(i, 1, 2)
+            if i + 1 < 8:
+                mix_copy(i + 1, 1)
+            if 0 < i and i + 3 < 8:
+                turn_mm(i + 3, 0)
+            if 0 < i and i + 3 < 8:
+                turn_copy(i + 3, 0, "s")
+            if i + 1 < 8:
                 mix(i + 1, 0)
-                finish(i, 1)
-                coarse(i + 1, 1)
+            if i + 1 < 8:
+                sk_t(i + 1, 1, 3)
+            if i + 1 < 8:
                 open_z(i + 1, 1)
-                pool_add(i + 1, 1)
+            if True:
+                if i + 1 < 8:
+                    finish(i, 1)
+                else:
+                    finish(i, 1, 0, 2)
+                    finish(i, 1, 2, 4)
+            if i + 1 < 8:
+                coarse(i + 1, 1)
+            if i + 1 < 8:
+                copy_coarse(i + 1, 1)
+            if i + 1 < 8:
+                g_add(i + 1, 1)
+            if True:
+                if i + 1 < 8:
+                    add_coarse(i, 0)
+                else:
+                    add_coarse(i, 0, 0, 2)
+                    add_coarse(i, 0, 2, 4)
+            if 0 < i and i + 3 < 8:
+                turn_mm(i + 3, 1)
+            if 0 < i and i + 3 < 8:
+                turn_copy(i + 3, 1, "s")
+            if i + 1 < 8:
                 mix_copy(i + 1, 0)
-            else:
-                finish(i, 1, 2, 4)
-            if far and i > 0:
-                turn_x(i + 3, 1, "s")
-            if nxt:
-                add_coarse(i, 0)
-                finish(i, 0)
-            else:
-                for j0 in (0, 2):
-                    add_coarse(i, 0, j0, j0 + 2)
-                    finish(i, 0, j0, j0 + 2)
-            if nxt:
-                early_part(i + 1, 1, SHARE)
-            for part in range(4):
-                if nxt and i > 0:
-                    early_part(i + 1, 0, part)
-                if mid:
-                    sum0_part(i + 2, part)
-            if nxt:
-                coarse(i + 1, 0)
-            if far:
-                turn_x(i + 3, 2, "s")
-            if nxt:
-                skip_ahead(i + 1, 1, 0)
-                skip_ahead(i + 1, 1, 1)
-            if far:
-                turn_x(i + 3, 3, "s")
-            if mid:
-                make_a(i + 2)
-            if mid and i > 0:
+            if i + 1 < 8:
+                sk_v(i + 1, 1, 3)
+            if 0 < i < 7:
+                sk_t(i + 1, 0, 0)
+            if 0 < i < 7:
+                sk_v(i + 1, 0, 0)
+            if 0 < i < 7:
+                sk_t(i + 1, 0, 1)
+            if 0 < i < 7:
+                sk_v(i + 1, 0, 1)
+            if True:
+                if i + 1 < 8:
+                    finish(i, 0)
+                else:
+                    finish(i, 0, 0, 2)
+                    finish(i, 0, 2, 4)
+            if 0 < i and i + 2 < 8:
                 quant_x(i + 2)
+            if 0 < i < 7:
+                sk_t(i + 1, 0, 2)
+            if 0 < i < 7:
+                sk_v(i + 1, 0, 2)
+            if 0 < i < 7:
+                sk_t(i + 1, 0, 3)
+            if 0 < i < 7:
+                sk_v(i + 1, 0, 3)
+            if i + 2 < 8:
+                sum0(i + 2)
+            if i + 3 < 8:
+                turn_mm(i + 3, 2)
+            if i + 3 < 8:
+                turn_copy(i + 3, 2, "s")
+            if i + 3 < 8:
+                turn_mm(i + 3, 3)
+            if i + 3 < 8:
+                turn_copy(i + 3, 3, "s")
+            if i + 1 < 8:
+                sk_t(i + 1, 1, 0)
+            if i + 1 < 8:
+                sk_t(i + 1, 1, 1)
+            if i + 1 < 8:
+                coarse(i + 1, 0)
+            if i + 2 < 8:
+                make_a(i + 2)
+            if i + 2 < 8:
+                quant_a(i + 2)

from contextlib import ExitStack

import concourse.mybir as mybir
from concourse.masks import make_identity

F32 = mybir.dt.float32
BF16 = mybir.dt.bfloat16
U32 = mybir.dt.uint32
U8 = mybir.dt.uint8
FP8X4 = mybir.dt.float8_e4m3fn_x4
ALU = mybir.AluOpType
ACT = mybir.ActivationFunctionType

P = 128
C = 512
UNITS = 8
R = 0.7071067811865476
R3 = R * R * R
SHARE = 3
FLOPS = 2 * 8192 * 512 * 512 + 2 * 2 * 8 * 128 * 512 * 512


def tile_waveletblock1d_t_kernel(tc, x, w_approx, w_detail, W_skip, b_skip, out):
    nc = tc.nc
    with ExitStack() as ctx:
        ctx.enter_context(tc.manual_schedule())
        const = ctx.enter_context(tc.tile_pool(name="const", bufs=1))
        pool1 = ctx.enter_context(tc.tile_pool(name="pool1", bufs=1))
        pool2 = ctx.enter_context(tc.tile_pool(name="pool2", bufs=2))
        pool3 = ctx.enter_context(tc.tile_pool(name="pool3", bufs=3))
        pool4 = ctx.enter_context(tc.tile_pool(name="pool4", bufs=3))
        xpool = ctx.enter_context(tc.tile_pool(name="xpool", bufs=4))
        ps_2 = ctx.enter_context(tc.psum_pool(name="ps_2", bufs=2))
        ps_4 = ctx.enter_context(tc.psum_pool(name="ps_4", bufs=4))

        warm = const.tile([P, 1], F32, name="warm")
        nc.vector.memset(warm[:], 0.0)
        nc.scalar.activation(out=warm[:], in_=warm[:], func=ACT.Gelu_apprx_tanh)
        ident = const.tile([P, P], F32, name="ident")
        make_identity(nc, ident[:])
        ident_b = const.tile([P, P], BF16, name="ident_b")
        make_identity(nc, ident_b[:])
        bias_b = const.tile([P, C], BF16, name="bias_b")
        bias_c = const.tile([P, 4], F32, name="bias_c")
        ws_codes = const.tile([P, C], U32, align_bytes=64, name="ws_codes")
        ws_scales = const.tile([P, C], U8, align_bytes=64, name="ws_scales")
        w_codes = [[[None, None], [None, None]], [[None, None], [None, None]]]
        w_scales = [[[None, None], [None, None]], [[None, None], [None, None]]]
        for s in range(2):
            for oh in range(2):
                for lh in range(2):
                    wc = const.tile([P, 1024], U32, align_bytes=64, name="wc%d%d%d" % (s, oh, lh))
                    wsc = const.tile([P, 1024], U8, align_bytes=64, name="wsc%d%d%d" % (s, oh, lh))
                    w_codes[s][oh][lh] = wc
                    w_scales[s][oh][lh] = wsc

        xus = {}
        xgs = {}
        tins = {}
        mixed = {}
        ahead = {}
        xqs = {}
        s0ps = {}
        s0s = {}
        s1s = {}
        s1rs = {}
        aqs = {}
        cts = {}
        cps = {}
        gqs = {}
        ccs = {}
        zs = {}

        def load_x(u, j0=0, j1=8):
            if j0 == 0:
                xu = xpool.tile([P, 8 * C], BF16, tag="xu", name="xu%d" % u)
                xus[u] = xu
            nc.sync.dma_start(
                out=xus[u][:, j0 * C : j1 * C], in_=x[:, 8 * u + j0 : 8 * u + j1, :].rearrange("b l c -> b (l c)")
            )

        def turn_mm(u, jp):
            if jp == 0:
                xg = pool2.tile([P, 8 * C], BF16, align_bytes=64, tag="xg", name="xg%d" % u)
                xgs[u] = xg
            xw = xus[u][:].bitcast(F32)
            tin = ps_4.tile([P, C], F32, tag="io", name="tin%d_%d" % (u, jp))
            for jj in range(2):
                j = 2 * jp + jj
                for uu in range(2):
                    nc.tensor.transpose(
                        tin[:, uu * 256 + jj * P : uu * 256 + jj * P + P],
                        xw[:, j * 256 + uu : (j + 1) * 256 : 2],
                        ident[:],
                    )
            tins[u, jp] = tin

        def turn_copy(u, jp, engine):
            tin = tins[u, jp]
            dst = xgs[u][:].bitcast(F32)[:, jp * C : (jp + 1) * C].rearrange("p (n u) -> p n u", u=2)
            srcv = tin[:].rearrange("p (u n) -> p n u", u=2)
            if engine == "v":
                nc.vector.tensor_copy(out=dst, in_=srcv)
            else:
                nc.scalar.copy(out=dst, in_=srcv)

        def turn_x(u, jp, engine):
            turn_mm(u, jp)
            turn_copy(u, jp, engine)

        def quant_x(u):
            xc = pool4.tile([P, 8 * P], U32, align_bytes=64, tag="xc", name="xc%d" % u)
            xs = pool4.tile([P, 8 * P], U8, align_bytes=64, tag="xs", name="xs%d" % u)
            nc.vector.quantize_mx(out=xc[:].bitcast(FP8X4), scales=xs[:], in_=xgs[u][:])
            xqs[u] = (xc, xs)

        def sum0_part(u, j):
            if j == 0:
                s0p = ps_2.tile([P, C], F32, tag="ms", name="s0p%d" % u)
                s0ps[u] = s0p
            nc.tensor.matmul(
                s0ps[u][:], ident_b[:], xgs[u][:, j * C : (j + 1) * C], start=(j == 0), stop=(j == 3)
            )

        def sum0(u):
            for j in range(4):
                sum0_part(u, j)

        def keep0(u):
            s0 = pool2.tile([P, C], F32, tag="s0", name="s0_%d" % u)
            nc.scalar.copy(
                out=s0[:].rearrange("p (t b) -> p t b", t=4), in_=s0ps[u][:].rearrange("p (b t) -> p t b", t=4)
            )
            s0s[u] = s0

        def sum1(u):
            xv = xgs[u][:, 4 * C : 8 * C].rearrange("p (k two c) -> p k two c", two=2, c=C)
            pp = pool1.tile([P, 2 * C], F32, tag="pp", name="pp%d" % u)
            for k in range(2):
                nc.gpsimd.tensor_tensor(
                    out=pp[:, k * C : (k + 1) * C], in0=xv[:, k, 0], in1=xv[:, k, 1], op=ALU.add
                )
            s1 = pool2.tile([P, C], F32, tag="s1", name="s1_%d" % u)
            nc.gpsimd.tensor_tensor(out=s1[:], in0=pp[:, 0:C], in1=pp[:, C : 2 * C], op=ALU.add)
            s1s[u] = s1
            s1r = pool1.tile([P, C], F32, tag="s1r", name="s1r%d" % u)
            nc.gpsimd.tensor_scalar(out=s1r[:], in0=s1[:], scalar1=R3, scalar2=0.0, op0=ALU.mult, op1=ALU.add)
            s1rs[u] = s1r

        def make_a(u):
            s1r = s1rs[u]
            gq = pool2.tile([P, 3 * C], BF16, align_bytes=64, tag="gq", name="gq%d" % u)
            for s in (1, 0):
                nc.vector.scalar_tensor_tensor(
                    out=gq[:, s * C : (s + 1) * C],
                    in0=s0ps[u][:],
                    scalar=R3,
                    in1=s1r[:],
                    op0=ALU.mult,
                    op1=(ALU.add, ALU.subtract)[s],
                )
            nc.vector.tensor_scalar(
                out=gq[:, 2 * C : 3 * C], in0=gq[:, C : 2 * C], scalar1=-1.0, scalar2=None, op0=ALU.mult
            )
            gqs[u] = gq

        def quant_a(u):
            gq = gqs[u]
            ac = pool2.tile([P, 3 * P], U32, align_bytes=64, tag="ac", name="ac%d" % u)
            asc = pool2.tile([P, 3 * P], U8, align_bytes=64, tag="as", name="as%d" % u)
            nc.vector.quantize_mx(out=ac[:, 0 : 2 * P].bitcast(FP8X4), scales=asc[:, 0 : 2 * P], in_=gq[:, 0 : 2 * C])
            nc.vector.quantize_mx(
                out=ac[:, 2 * P : 3 * P].bitcast(FP8X4), scales=asc[:, 2 * P : 3 * P], in_=gq[:, 2 * C : 3 * C]
            )
            aqs[u] = (ac, asc)

        def mix(u, h):
            ac, asc = aqs[u]
            lh, li = divmod(u, 4)
            mx = ps_2.tile([P, C], F32, tag="ms", name="mix%d_%d" % (u, h))
            for ob in range(4):
                w0 = (ob % 2) * 512 + li * P
                for s in range(2):
                    a0 = (0, 1 + h)[s] * P
                    nc.tensor.matmul_mx(
                        out=mx[:, ob * P : (ob + 1) * P],
                        lhsT=w_codes[s][ob // 2][lh][:, w0 : w0 + P].bitcast(FP8X4),
                        lhsT_scale=w_scales[s][ob // 2][lh][:, w0 : w0 + P],
                        rhs=ac[:, a0 : a0 + P].bitcast(FP8X4),
                        rhs_scale=asc[:, a0 : a0 + P],
                        start=(s == 0),
                        stop=(s == 1),
                    )
            mixed[u, h] = mx

        def mix_copy(u, h):
            ct = pool2.tile([P, C], F32, tag="ct", name="ct%d_%d" % (u, h))
            for ob in range(4):
                cols = slice(ob * P, (ob + 1) * P)
                nc.scalar.activation(
                    out=ct[:, cols],
                    in_=mixed[u, h][:, cols],
                    func=ACT.Identity,
                    scale=-4.0 * R3,
                    bias=bias_c[:, ob : ob + 1],
                )
            cts[u, h] = ct

        def coarse(u, h):
            cp = ps_2.tile([P, C], F32, tag="cp", name="cp%d_%d" % (u, h))
            for ob in range(4):
                nc.tensor.matmul(
                    cp[:, ob * P : (ob + 1) * P],
                    cts[u, h][:, ob * P : (ob + 1) * P],
                    ident[:],
                    start=(ob == 0),
                    stop=False,
                    is_transpose=True,
                )
            for t in range(4):
                nc.tensor.matmul(
                    cp[:, t : C : 4],
                    s0s[u][:, t * P : (t + 1) * P] if h == 0 else s1s[u][:, t : C : 4],
                    ident[:],
                    start=False,
                    stop=(t == 3),
                    is_transpose=True,
                )
            cps[u, h] = cp

        def skip(u, j):
            sk = ps_4.tile([P, C], F32, tag="io", name="sk%d_%d" % (u, j))
            xc, xs = xqs[u]
            nc.tensor.matmul_mx(
                out=sk[:],
                lhsT=xc[:, j * P : (j + 1) * P].bitcast(FP8X4),
                lhsT_scale=xs[:, j * P : (j + 1) * P],
                rhs=ws_codes[:].bitcast(FP8X4),
                rhs_scale=ws_scales[:],
                start=True,
                stop=True,
            )
            return sk

        def open_z(u, h):
            if h == 1 and u > 0:
                z = zpool.tile([P, 4 * C], F32, tag="z", name="z%d" % u)
            else:
                z = pool3.tile([P, 4 * C], F32, tag="t", name="t%d_%d" % (u, h))
            zs[u, h] = z

        def early_part(u, h, jj):
            if (u, h) not in zs:
                open_z(u, h)
            j = 4 * h + jj
            sk = skip(u, j)
            nc.vector.tensor_tensor(
                out=zs[u, h][:, jj * C : (jj + 1) * C], in0=sk[:], in1=xus[u][:, j * C : (j + 1) * C], op=ALU.add
            )

        def early(u, h):
            for jj in range(4):
                early_part(u, h, jj)

        def wide(ap, n):
            return ap.unsqueeze(1).to_broadcast([P, n, C])

        def sk_t(u, h, jj):
            ahead[u, h, jj] = skip(u, 4 * h + jj)

        def sk_v(u, h, jj):
            if (u, h) not in zs:
                open_z(u, h)
            j = 4 * h + jj
            cols = slice(jj * C, (jj + 1) * C)
            if h == 1 and u > 0 and jj < SHARE:
                other = zs[u, h][:, cols]
            else:
                other = xus[u][:, j * C : (j + 1) * C]
            nc.vector.tensor_tensor(out=zs[u, h][:, cols], in0=ahead[u, h, jj][:], in1=other, op=ALU.add)

        def copy_coarse(u, h):
            cc = pool2.tile([P, C], F32, tag="cc", name="cc%d" % u)
            nc.scalar.mul(cc[:], cps[u, h][:], -0.25)
            ccs[u, h] = cc

        def g_add(u, h):
            z = zs[u, h]
            for jj in range(SHARE):
                j = 4 * h + jj
                nc.gpsimd.tensor_tensor(
                    out=z[:, jj * C : (jj + 1) * C], in0=xus[u][:, j * C : (j + 1) * C], in1=ccs[u, h][:], op=ALU.add
                )

        def add_coarse(u, h, j0=0, j1=4):
            z4 = zs[u, h][:, j0 * C : j1 * C].rearrange("p (j c) -> p j c", c=C)
            nc.vector.scalar_tensor_tensor(
                out=z4, in0=wide(cps[u, h][:], j1 - j0), scalar=-0.25, in1=z4, op0=ALU.mult, op1=ALU.add
            )

        def pool_add(u, h):
            cc = pool2.tile([P, C], F32, tag="cc", name="cc%d" % u)
            nc.scalar.mul(cc[:], cps[u, h][:], -0.25)
            z = zs[u, h]
            for jj in range(SHARE):
                j = 4 * h + jj
                nc.gpsimd.tensor_tensor(
                    out=z[:, jj * C : (jj + 1) * C], in0=xus[u][:, j * C : (j + 1) * C], in1=cc[:], op=ALU.add
                )
            zs[u, h] = z

        def skip_ahead(u, h, jj):
            ahead[u, h, jj] = skip(u, 4 * h + jj)

        def add_skip_part(u, h, jj):
            z = zs[u, h]
            sk = ahead[u, h, jj] if (u, h, jj) in ahead else skip(u, 4 * h + jj)
            nc.vector.tensor_tensor(
                out=z[:, jj * C : (jj + 1) * C], in0=sk[:], in1=z[:, jj * C : (jj + 1) * C], op=ALU.add
            )

        def finish(u, h, j0=0, j1=4):
            z = zs[u, h][:, j0 * C : j1 * C]
            nc.scalar.activation(out=z, in_=z, func=ACT.Gelu_apprx_tanh)
            l0 = 8 * u + 4 * h
            nc.sync.dma_start(out=out[:, l0 + j0 : l0 + j1, :].rearrange("b l o -> b (l o)"), in_=z)

        with tc.tile_pool(name="wstage", bufs=5) as wstage, tc.tile_pool(name="wraw", bufs=4) as rawpool:
            raws = {}
            wgs = {}

            def load_w(g, i):
                s, oh = divmod(g, 2)
                oq = 2 * oh + i
                raw = rawpool.tile([P, 4 * P * 8], BF16, tag="raw", name="raw%d_%d" % (g, i))
                nc.sync.dma_start(
                    out=raw[:].rearrange("p (t r) -> p t r", t=4),
                    in_=(w_approx, w_detail)[s]
                    .rearrange("(p t) o l -> p t o l", t=4)[:, :, oq * P : (oq + 1) * P, :]
                    .rearrange("p t o l -> p t (o l)"),
                )
                raws[g, i] = raw

            def lay_w(g, i, lh, engine):
                if i == 0:
                    wg = wstage.tile([P, 4096], BF16, align_bytes=64, tag="wg", name="wg%d_%d" % (g, lh))
                    wgs[g, lh] = wg
                srcv = raws[g, i][:].rearrange("p (t o l) -> p o t l", t=4, l=8)[:, :, :, 4 * lh : 4 * lh + 4]
                dstv = wgs[g, lh][:, i * 2048 : (i + 1) * 2048].rearrange("p (l o t) -> p o t l", l=4, t=4)
                if engine == "v":
                    nc.vector.tensor_copy(out=dstv, in_=srcv)
                elif engine == "g":
                    nc.gpsimd.tensor_scalar(
                        out=dstv.rearrange("p o t l -> p o l t"),
                        in0=srcv.rearrange("p o t l -> p o l t"),
                        scalar1=1.0,
                        scalar2=0.0,
                        op0=ALU.mult,
                        op1=ALU.add,
                    )
                else:
                    nc.scalar.copy(out=dstv, in_=srcv)

            def quant_w(g, lh):
                s, oh = divmod(g, 2)
                nc.vector.quantize_mx(
                    out=w_codes[s][oh][lh][:].bitcast(FP8X4), scales=w_scales[s][oh][lh][:], in_=wgs[g, lh][:]
                )

            def bias_col():
                bias = pool2.tile([P, C], F32, tag="ct", name="bias")
                nc.vector.tensor_copy(out=bias[:], in_=bias_b[:])
                bp = ps_4.tile([P, C], F32, tag="io", name="bp")
                for ob in range(4):
                    nc.tensor.transpose(bp[:, ob * P : (ob + 1) * P], bias[:, ob * P : (ob + 1) * P], ident[:])
                nc.scalar.mul(bias_c[:], bp[:, 0:C:P], -4.0)

            def quant_skip():
                wsg = wsraw[:, 4 * C : 8 * C]
                nc.vector.tensor_copy(
                    out=wsg.rearrange("p (o t) -> p o t", t=4),
                    in_=wsraw[:, 0 : 4 * C].rearrange("p (t o) -> p o t", t=4),
                )
                nc.vector.quantize_mx(out=ws_codes[:].bitcast(FP8X4), scales=ws_scales[:], in_=wsg)

            load_x(0, 0, 4)
            wsraw = pool2.tile([P, 8 * C], BF16, align_bytes=64, tag="xg", name="wsraw")
            nc.sync.dma_start(
                out=wsraw[:, 0 : 4 * C].rearrange("p (t o) -> p t o", t=4),
                in_=W_skip.rearrange("(q t) o -> q t o", t=4),
            )
            load_x(0, 4, 8)
            load_w(0, 0)
            nc.sync.dma_start(out=bias_b[:], in_=b_skip.partition_broadcast(P))
            load_w(0, 1)
            load_w(1, 0)
            load_w(1, 1)
            load_x(1)

            turn_x(0, 0, "s")
            turn_x(0, 1, "s")
            quant_skip()
            turn_x(0, 2, "v")
            turn_x(0, 3, "v")
            quant_x(0)
            sum0(0)
            sum1(0)
            lay_w(0, 0, 0, "s")
            lay_w(0, 0, 1, "s")
            load_w(2, 0)
            early(0, 0)
            bias_col()
            lay_w(0, 1, 0, "s")
            lay_w(0, 1, 1, "v")
            load_w(2, 1)
            load_x(2)
            early(0, 1)
            lay_w(1, 0, 0, "s")
            quant_w(0, 0)
            make_a(0)
            quant_a(0)
            lay_w(1, 0, 1, "s")
            load_w(3, 0)
            quant_w(0, 1)
            keep0(0)
            lay_w(1, 1, 0, "g")
            lay_w(1, 1, 1, "v")
            load_w(3, 1)
            load_x(3)
            turn_x(1, 0, "s")
            turn_x(1, 1, "v")
            quant_w(1, 0)
            turn_x(1, 2, "v")
            turn_x(1, 3, "v")
            quant_w(1, 1)
            quant_x(1)
            sum0(1)
            sum1(1)
            lay_w(2, 0, 0, "s")
            lay_w(2, 0, 1, "s")
            lay_w(2, 1, 0, "s")
            lay_w(2, 1, 1, "v")
            turn_x(2, 0, "v")
            turn_x(2, 1, "v")
            quant_w(2, 0)
            turn_x(2, 2, "v")
            turn_x(2, 3, "v")
            lay_w(3, 0, 0, "s")
            lay_w(3, 1, 0, "s")
            make_a(1)
            quant_a(1)
            keep0(1)
            quant_w(3, 0)
            quant_w(2, 1)
            sum1(2)
            turn_x(3, 0, "s")
            turn_x(3, 1, "s")
            mix(0, 1)
            mix_copy(0, 1)
            early_part(1, 0, 0)
            early_part(1, 0, 1)
            mix(0, 0)
            mix_copy(0, 0)
            early_part(1, 0, 2)
            early_part(1, 0, 3)
            lay_w(3, 0, 1, "s")
            lay_w(3, 1, 1, "v")
            quant_x(2)
            quant_w(3, 1)
            coarse(0, 1)
            coarse(0, 0)

        zpool = ctx.enter_context(tc.tile_pool(name="zpool", bufs=4))

        for i in range(UNITS):
            nxt, mid, far = i + 1 < UNITS, i + 2 < UNITS, i + 3 < UNITS
            if i + 4 < 8:
                load_x(i + 4)
            if 0 < i and i + 2 < 8:
                sum1(i + 2)
            if i > 0:
                sk_t(i, 1, 2)
            if i + 1 < 8:
                mix(i + 1, 1)
            if i + 1 < 8 and i > 0:
                keep0(i + 1)
            if True:
                add_coarse(i, 1, SHARE if i > 0 else 0, 4)
            if i > 0:
                sk_v(i, 1, 0)
            if i > 0:
                sk_v(i, 1, 1)
            if i > 0:
                sk_v(i, 1, 2)
            if i + 1 < 8:
                mix_copy(i + 1, 1)
            if 0 < i and i + 3 < 8:
                turn_mm(i + 3, 0)
            if 0 < i and i + 3 < 8:
                turn_copy(i + 3, 0, "s")
            if i + 1 < 8:
                mix(i + 1, 0)
            if i + 1 < 8:
                sk_t(i + 1, 1, 3)
            if i + 1 < 8:
                open_z(i + 1, 1)
            if True:
                if i + 1 < 8:
                    finish(i, 1)
                else:
                    finish(i, 1, 0, 2)
                    finish(i, 1, 2, 4)
            if i + 1 < 8:
                coarse(i + 1, 1)
            if i + 1 < 8:
                copy_coarse(i + 1, 1)
            if i + 1 < 8:
                g_add(i + 1, 1)
            if True:
                if i + 1 < 8:
                    add_coarse(i, 0)
                else:
                    add_coarse(i, 0, 0, 2)
                    add_coarse(i, 0, 2, 4)
            if 0 < i and i + 3 < 8:
                turn_mm(i + 3, 1)
            if 0 < i and i + 3 < 8:
                turn_copy(i + 3, 1, "s")
            if i + 1 < 8:
                mix_copy(i + 1, 0)
            if i + 1 < 8:
                sk_v(i + 1, 1, 3)
            if 0 < i < 7:
                sk_t(i + 1, 0, 0)
            if 0 < i < 7:
                sk_v(i + 1, 0, 0)
            if 0 < i < 7:
                sk_t(i + 1, 0, 1)
            if 0 < i < 7:
                sk_v(i + 1, 0, 1)
            if True:
                if i + 1 < 8:
                    finish(i, 0)
                else:
                    finish(i, 0, 0, 2)
                    finish(i, 0, 2, 4)
            if 0 < i and i + 2 < 8:
                quant_x(i + 2)
            if 0 < i < 7:
                sk_t(i + 1, 0, 2)
            if 0 < i < 7:
                sk_v(i + 1, 0, 2)
            if 0 < i < 7:
                sk_t(i + 1, 0, 3)
            if 0 < i < 7:
                sk_v(i + 1, 0, 3)
            if i + 2 < 8:
                sum0(i + 2)
            if i + 3 < 8:
                turn_mm(i + 3, 2)
            if i + 3 < 8:
                turn_copy(i + 3, 2, "s")
            if i + 3 < 8:
                turn_mm(i + 3, 3)
            if i + 3 < 8:
                turn_copy(i + 3, 3, "s")
            if i + 1 < 8:
                sk_t(i + 1, 1, 0)
            if i + 1 < 8:
                sk_t(i + 1, 1, 1)
            if i + 1 < 8:
                coarse(i + 1, 0)
            if i + 2 < 8:
                make_a(i + 2)
            if i + 2 < 8:
                quant_a(i + 2)
